import numpy as np
import ml_dtypes


def mxq(x, axis, fmt="e4m3"):
    dtype, down = {"e4m3": (ml_dtypes.float8_e4m3fn, 7), "e5m2": (ml_dtypes.float8_e5m2, 14)}[fmt]
    v = np.moveaxis(np.asarray(x, np.float32).astype(ml_dtypes.bfloat16).astype(np.float64), axis, -1)
    blocks = v.reshape(v.shape[:-1] + (-1, 32))
    amax = np.abs(blocks).max(-1, keepdims=True)
    byte = np.maximum(np.where(amax > 0, np.frexp(amax)[1] - 1 + 127, 0) - down, 1)
    scale = np.exp2(byte - 127.0)
    codes = (blocks / scale).astype(np.float32).astype(dtype).astype(np.float64)
    return np.moveaxis((codes * scale).reshape(v.shape), -1, axis)


WIDE = False


def mx_kscale(k):
    if not WIDE:
        return np.ones(k)
    levels = np.array([10, -10, 5, -5, 0])
    a = np.random.permutation(np.resize(levels, k // 512 * 4)).reshape(k // 512, 4)
    idx = np.arange(k)
    return np.exp2(a[idx // 512, idx % 128 // 32])


BF16 = ml_dtypes.bfloat16


def bf(x):
    return np.asarray(x, np.float32).astype(BF16)


def f64(x):
    return np.asarray(x).astype(np.float64)


B, GRID, PATCH, D, NH, NCLS = 128, 6, 16, 512, 16, 1000
N = GRID * GRID + 1
D3 = 3 * D
EPS = 1e-5


def layernorm(v, g, b):
    mu = v.mean(-1, keepdims=True)
    var = ((v - mu) ** 2).mean(-1, keepdims=True)
    return (v - mu) / np.sqrt(var + EPS) * g + b


def setup_inputs():
    s = mx_kscale(D)
    return {
        "attn_l": bf(np.random.standard_normal((B, N, D)) * s),
        "wo_l": bf(np.random.standard_normal((D, D)) / np.sqrt(D) / s),
        "bo_l": bf(np.random.standard_normal(D) * 0.1),
        "g1": bf(1.0 + np.random.standard_normal(D) * 0.1),
        "be1": bf(np.random.standard_normal(D) * 0.1),
        "wqkv_g": bf(np.random.standard_normal((D3, D)) / np.sqrt(D)),
        "bqkv_g": bf(np.random.standard_normal(D3) * 0.1),
    }


def reference(attn_l, wo_l, bo_l, g1, be1, wqkv_g, bqkv_g):
    y = (mxq(f64(attn_l), 2, "e4m3") @ mxq(f64(wo_l), 1, "e4m3").T) + f64(bo_l)
    local = layernorm(y, f64(g1), f64(be1))
    return (mxq(local, 2, "e4m3") @ mxq(f64(wqkv_g), 1, "e4m3").T) + f64(bqkv_g)

@@ -1,0 +1,297 @@
+from contextlib import ExitStack
+
+import concourse.mybir as mybir
+from concourse.masks import make_identity
+
+F32 = mybir.dt.float32
+BF16 = mybir.dt.bfloat16
+U32 = mybir.dt.uint32
+U8 = mybir.dt.uint8
+FP8X4 = mybir.dt.float8_e4m3fn_x4
+ALU = mybir.AluOpType
+ACT = mybir.ActivationFunctionType
+
+P = 128
+PACK = 4
+D = 512
+D3 = 1536
+BANK = 512
+TOKENS = 128 * 37
+TILES = TOKENS // P
+GROUP = 2
+EPS = 1e-5
+
+FLOPS = 2 * TOKENS * D * (D + D3)
+
+X_AT = 0
+XQ_AT = 2
+Y_AT = 3
+SQ_AT = 4
+RSTD_AT = 6
+Z_AT = 7
+ZT_AT = 9
+LQ_AT = 11
+OUT_AT = 12
+
+
+def transpose_rows(nc, banks, stage, ident, row_tiles):
+    n = len(row_tiles)
+    grouped = stage.tile([P, n * P * PACK], BF16, align_bytes=64, tag="grouped")
+    words = grouped[:].bitcast(F32).rearrange("p (r u) -> p r u", u=2)
+    for first in range(0, n, 2):
+        pair = row_tiles[first : first + 2]
+        m = len(pair)
+        bank = banks.tile([P, 2, 2, P], F32, tag="s")
+        for r in range(m):
+            for u in range(2):
+                nc.tensor.transpose(
+                    out=bank[:, r, u, :], in_=pair[r][:, u * P : (u + 1) * P], identity=ident[:]
+                )
+        nc.scalar.copy(
+            out=words[:, first * P : (first + m) * P, :].rearrange("p (r c) u -> p r c u", r=m),
+            in_=bank[:, :m, :, :].rearrange("p r u c -> p r c u"),
+        )
+    return grouped
+
+
+def tile_hlgan_pb_t_kernel(tc, attn_l, wo_l, bo_l, g1, be1, wqkv_g, bqkv_g, out):
+    nc = tc.nc
+    x_dram = attn_l.flatten_outer_dims().rearrange("(p j) d -> p j d", j=TILES)
+    out_dram = out.flatten_outer_dims().rearrange("(p j) f -> p j f", j=TILES)
+    sizes = [min(GROUP, TILES - j0) for j0 in range(0, TILES, GROUP)]
+    n_groups = len(sizes)
+
+    def tile_at(step, lag):
+        g, q = divmod(step - lag, GROUP)
+        if 0 <= g < n_groups and q < sizes[g]:
+            return g, q
+        return None
+
+    def group_at(step, lag):
+        g, q = divmod(step - lag, GROUP)
+        if 0 <= g < n_groups and q == 0:
+            return g
+        return None
+
+    with ExitStack() as ctx:
+        const = ctx.enter_context(tc.tile_pool(name="const", bufs=1))
+        stage = ctx.enter_context(tc.tile_pool(name="stage", bufs=3))
+        q_pool = ctx.enter_context(tc.tile_pool(name="q", bufs=3))
+        y_pool = ctx.enter_context(tc.tile_pool(name="y", bufs=6))
+        stat = ctx.enter_context(tc.tile_pool(name="stat", bufs=6))
+        scratch = ctx.enter_context(tc.tile_pool(name="scratch", bufs=4))
+        l_pool = ctx.enter_context(tc.tile_pool(name="l", bufs=3))
+        o_pool = ctx.enter_context(tc.tile_pool(name="o", bufs=4))
+        psum_v = ctx.enter_context(tc.psum_pool(name="psum_v", bufs=4))
+        psum_s = ctx.enter_context(tc.psum_pool(name="psum_s", bufs=4))
+        ctx.enter_context(tc.manual_schedule())
+
+        wo_sb = const.tile([P, 4, D], BF16)
+        for u in range(2):
+            nc.sync.dma_start(
+                out=wo_sb[:, 2 * u : 2 * u + 2, :],
+                in_=wo_l[256 * u : 256 * (u + 1), :].rearrange("(q e) k -> q e k", e=2),
+            )
+        x_sb = []
+        wqkv_sb = const.tile([P, D3 // P, D], BF16)
+        for g in range(n_groups):
+            x_g = const.tile([P, sizes[g], D], BF16, name="x_%d" % g)
+            nc.sync.dma_start(out=x_g[:], in_=x_dram[:, g * GROUP : g * GROUP + sizes[g], :])
+            x_sb.append(x_g)
+            if g == 1:
+                nc.sync.dma_start(out=wqkv_sb[:], in_=wqkv_g.rearrange("(r q) k -> q r k", q=P))
+
+        bo_bf = const.tile([P, D], BF16)
+        nc.scalar.dma_start(out=bo_bf[:], in_=bo_l.partition_broadcast(P))
+        gb_rows = const.tile([P, 2 * P], BF16)
+        nc.vector.memset(gb_rows[:], 0.0)
+        nc.scalar.dma_start(out=gb_rows[0:2, :], in_=g1.rearrange("(u w) -> u w", u=2))
+        nc.scalar.dma_start(out=gb_rows[2:4, :], in_=be1.rearrange("(u w) -> u w", u=2))
+        bq_bf = const.tile([P, D3], BF16)
+        nc.scalar.dma_start(out=bq_bf[:], in_=bqkv_g.partition_broadcast(P))
+
+        eps = const.tile([P, 1], F32)
+        nc.vector.memset(eps[:], EPS)
+        warm = const.tile([P, 1], F32)
+        nc.scalar.activation(out=warm[:], in_=eps[:], func=ACT.Sqrt)
+        ident = const.tile([P, P], F32)
+        make_identity(nc, ident[:])
+
+        wo_q = const.tile([P, D], U32, align_bytes=64)
+        wo_s = const.tile([P, D], U8, align_bytes=64)
+        wo_words = wo_sb[:].bitcast(F32)
+        wo_grouped = transpose_rows(nc, psum_s, stage, ident, [wo_words[:, r, :] for r in range(4)])
+        nc.vector.quantize_mx(out=wo_q[:].bitcast(FP8X4), scales=wo_s[:], in_=wo_grouped[:])
+        wq_q = const.tile([P, D3], U32, align_bytes=64)
+        wq_s = const.tile([P, D3], U8, align_bytes=64)
+        wq_words = wqkv_sb[:].bitcast(F32)
+
+        bo_bc = const.tile([P, D], F32)
+        nc.vector.tensor_copy(
+            out=bo_bc[:].rearrange("p (u e q) -> p u e q", u=2, e=2),
+            in_=bo_bf[:].rearrange("p (u q e) -> p u e q", u=2, e=2),
+        )
+        bq_bc = const.tile([P, D3], F32)
+        nc.gpsimd.tensor_copy(out=bq_bc[:], in_=bq_bf[:])
+
+        gb_bank = psum_s.tile([P, P], F32, tag="s")
+        nc.tensor.transpose(out=gb_bank[:], in_=gb_rows[:].bitcast(F32), identity=ident[:])
+        gain_shift = const.tile([P, 2 * PACK], F32)
+        nc.vector.tensor_copy(out=gain_shift[:], in_=gb_bank[:, 0:4].bitcast(BF16))
+
+        x_grouped, xq, xs, yb, ysum, ssq, rstd, nbias, lt, lq, ls, o_sb = (
+            {}, {}, {}, {}, {}, {}, {}, {}, {}, {}, {}, {},
+        )
+
+        for step in range(GROUP * (n_groups - 1) + OUT_AT + GROUP):
+            g = group_at(step, XQ_AT)
+            if g is not None:
+                toks = sizes[g] * P
+                xq[g] = q_pool.tile([P, GROUP * P], U32, align_bytes=64, name="xq")
+                xs[g] = q_pool.tile([P, GROUP * P], U8, align_bytes=64, name="xs")
+                nc.vector.quantize_mx(
+                    out=xq[g][:, :toks].bitcast(FP8X4), scales=xs[g][:, :toks], in_=x_grouped[g][:]
+                )
+
+            g = group_at(step, LQ_AT)
+            if g is not None:
+                toks = sizes[g] * P
+                lg = l_pool.tile([P, GROUP * P, PACK], BF16, align_bytes=64)
+                nc.vector.tensor_copy(
+                    out=lg[:, :toks, :], in_=lt[g][:, :, :toks].rearrange("p t c -> p c t")
+                )
+                lq[g] = q_pool.tile([P, GROUP * P], U32, align_bytes=64, name="lq")
+                ls[g] = q_pool.tile([P, GROUP * P], U8, align_bytes=64, name="ls")
+                nc.vector.quantize_mx(
+                    out=lq[g][:, :toks].bitcast(FP8X4), scales=ls[g][:, :toks],
+                    in_=lg[:, :toks, :].rearrange("p c t -> p (c t)"),
+                )
+
+            gq = tile_at(step, Z_AT)
+            if gq is not None:
+                g, q = gq
+                nc.gpsimd.tensor_scalar(
+                    out=yb[g][:, q, :], in0=yb[g][:, q, :],
+                    scalar1=rstd[g][:, q : q + 1], scalar2=nbias[g][:, q : q + 1],
+                    op0=ALU.mult, op1=ALU.add,
+                )
+
+            gq = tile_at(step, OUT_AT)
+            if gq is not None:
+                g, q = gq
+                if q == 0:
+                    o_sb[g] = o_pool.tile([P, GROUP, D3], F32, name="o_sb")
+                tok = slice(q * P, (q + 1) * P)
+                for c in range(3):
+                    cols = slice(c * BANK, (c + 1) * BANK)
+                    if c < 2:
+                        acc = psum_v.tile([P, BANK], F32, tag="v")
+                    else:
+                        acc = psum_s.tile([P, BANK], F32, tag="s")
+                    nc.tensor.matmul_mx(
+                        out=acc[:],
+                        lhsT=lq[g][:, tok].bitcast(FP8X4),
+                        lhsT_scale=ls[g][:, tok],
+                        rhs=wq_q[:, cols].bitcast(FP8X4),
+                        rhs_scale=wq_s[:, cols],
+                        start=True,
+                        stop=True,
+                    )
+                    if c < 2:
+                        nc.vector.tensor_tensor(
+                            out=o_sb[g][:, q, cols], in0=acc[:], in1=bq_bc[:, cols], op=ALU.add
+                        )
+                    else:
+                        nc.scalar.copy(out=o_sb[g][:, q, cols], in_=acc[:])
+                        nc.gpsimd.tensor_tensor(
+                            out=o_sb[g][:, q, cols], in0=o_sb[g][:, q, cols], in1=bq_bc[:, cols], op=ALU.add
+                        )
+                if q == sizes[g] - 1:
+                    nc.sync.dma_start(
+                        out=out_dram[:, g * GROUP : g * GROUP + sizes[g], :], in_=o_sb[g][:, : sizes[g], :]
+                    )
+
+            gq = tile_at(step, Y_AT)
+            if gq is not None:
+                g, q = gq
+                if q == 0:
+                    yb[g] = y_pool.tile([P, GROUP, D], F32, name="yb")
+                    ysum[g] = stat.tile([P, GROUP], F32, name="ysum")
+                y_ps = psum_v.tile([P, BANK], F32, tag="v")
+                nc.tensor.matmul_mx(
+                    out=y_ps[:],
+                    lhsT=xq[g][:, q * P : (q + 1) * P].bitcast(FP8X4),
+                    lhsT_scale=xs[g][:, q * P : (q + 1) * P],
+                    rhs=wo_q[:].bitcast(FP8X4),
+                    rhs_scale=wo_s[:],
+                    start=True,
+                    stop=True,
+                )
+                nc.vector.scalar_tensor_tensor(
+                    out=yb[g][:, q, :], in0=y_ps[:], scalar=1.0, in1=bo_bc[:],
+                    op0=ALU.mult, op1=ALU.add, accum_out=ysum[g][:, q : q + 1],
+                )
+
+            g, h = divmod(step - ZT_AT, GROUP)
+            if 0 <= g < n_groups:
+                n = sizes[g]
+                if h == 0:
+                    lt[g] = l_pool.tile([P, PACK, GROUP * P], BF16, name="lt")
+                zt = psum_s.tile([P, 2, GROUP * P], F32, tag="s")
+                for k in range(2):
+                    t = 2 * h + k
+                    for i in range(n):
+                        nc.tensor.transpose(
+                            out=zt[:, k, i * P : (i + 1) * P], in_=yb[g][:, i, t * P : (t + 1) * P],
+                            identity=ident[:],
+                        )
+                for k in range(2):
+                    t = 2 * h + k
+                    nc.scalar.activation(
+                        out=lt[g][:, t, : n * P], in_=zt[:, k, : n * P], func=ACT.Identity,
+                        bias=gain_shift[:, PACK + t : PACK + t + 1], scale=gain_shift[:, t : t + 1],
+                    )
+
+            g = group_at(step, X_AT)
+            if g is not None:
+                x_words = x_sb[g][:].bitcast(F32)
+                x_grouped[g] = transpose_rows(
+                    nc, psum_s, stage, ident, [x_words[:, i, :] for i in range(sizes[g])]
+                )
+
+            if 1 <= step <= 3:
+                c = step - 1
+                cols = slice(c * BANK, (c + 1) * BANK)
+                wq_grouped = transpose_rows(
+                    nc, psum_s, stage, ident, [wq_words[:, 4 * c + r, :] for r in range(4)]
+                )
+                nc.vector.quantize_mx(
+                    out=wq_q[:, cols].bitcast(FP8X4), scales=wq_s[:, cols], in_=wq_grouped[:]
+                )
+
+            gq = tile_at(step, SQ_AT)
+            if gq is not None:
+                g, q = gq
+                if q == 0:
+                    ssq[g] = stat.tile([P, GROUP], F32, name="ssq")
+                sq = scratch.tile([P, D], BF16)
+                nc.scalar.activation(
+                    out=sq[:], in_=yb[g][:, q, :], func=ACT.Square,
+                    bias=ysum[g][:, q : q + 1], scale=-float(D), accum_out=ssq[g][:, q : q + 1],
+                )
+                if q == sizes[g] - 1:
+                    n = sizes[g]
+                    nc.scalar.activation(
+                        out=ssq[g][:, :n], in_=ssq[g][:, :n], func=ACT.Sqrt, bias=eps[:], scale=1.0 / D**3
+                    )
+
+            g = group_at(step, RSTD_AT)
+            if g is not None:
+                n = sizes[g]
+                rstd[g] = stat.tile([P, GROUP], F32, name="rstd")
+                nc.vector.reciprocal(rstd[g][:, :n], ssq[g][:, :n])
+                nbias[g] = stat.tile([P, GROUP], F32, name="nbias")
+                nc.vector.scalar_tensor_tensor(
+                    out=nbias[g][:, :n], in0=ysum[g][:, :n], scalar=-1.0 / D, in1=rstd[g][:, :n],
+                    op0=ALU.mult, op1=ALU.mult,
+                )

@@ -170,7 +170,7 @@ def tile_hlgan_pb_t_kernel(tc, attn_l, wo_l, bo_l, g1, be1, wqkv_g, bqkv_g, out)
             gq = tile_at(step, Z_AT)
             if gq is not None:
                 g, q = gq
-                nc.gpsimd.tensor_scalar(
+                nc.vector.tensor_scalar(
                     out=yb[g][:, q, :], in0=yb[g][:, q, :],
                     scalar1=rstd[g][:, q : q + 1], scalar2=nbias[g][:, q : q + 1],
                     op0=ALU.mult, op1=ALU.add,

@@ -82,8 +82,8 @@ def tile_hlgan_pb_t_kernel(tc, attn_l, wo_l, bo_l, g1, be1, wqkv_g, bqkv_g, out)
         scratch = ctx.enter_context(tc.tile_pool(name="scratch", bufs=4))
         l_pool = ctx.enter_context(tc.tile_pool(name="l", bufs=3))
         o_pool = ctx.enter_context(tc.tile_pool(name="o", bufs=4))
-        psum_v = ctx.enter_context(tc.psum_pool(name="psum_v", bufs=4))
-        psum_s = ctx.enter_context(tc.psum_pool(name="psum_s", bufs=4))
+        psum_v = ctx.enter_context(tc.psum_pool(name="psum_v", bufs=5))
+        psum_s = ctx.enter_context(tc.psum_pool(name="psum_s", bufs=3))
         ctx.enter_context(tc.manual_schedule())
 
         wo_sb = const.tile([P, 4, D], BF16)
@@ -170,10 +170,9 @@ def tile_hlgan_pb_t_kernel(tc, attn_l, wo_l, bo_l, g1, be1, wqkv_g, bqkv_g, out)
             gq = tile_at(step, Z_AT)
             if gq is not None:
                 g, q = gq
-                nc.vector.tensor_scalar(
-                    out=yb[g][:, q, :], in0=yb[g][:, q, :],
-                    scalar1=rstd[g][:, q : q + 1], scalar2=nbias[g][:, q : q + 1],
-                    op0=ALU.mult, op1=ALU.add,
+                nc.scalar.activation(
+                    out=yb[g][:, q, :], in_=yb[g][:, q, :], func=ACT.Identity,
+                    bias=nbias[g][:, q : q + 1], scale=rstd[g][:, q : q + 1],
                 )
 
             gq = tile_at(step, OUT_AT)
@@ -184,10 +183,7 @@ def tile_hlgan_pb_t_kernel(tc, attn_l, wo_l, bo_l, g1, be1, wqkv_g, bqkv_g, out)
                 tok = slice(q * P, (q + 1) * P)
                 for c in range(3):
                     cols = slice(c * BANK, (c + 1) * BANK)
-                    if c < 2:
-                        acc = psum_v.tile([P, BANK], F32, tag="v")
-                    else:
-                        acc = psum_s.tile([P, BANK], F32, tag="s")
+                    acc = psum_v.tile([P, BANK], F32, tag="v")
                     nc.tensor.matmul_mx(
                         out=acc[:],
                         lhsT=lq[g][:, tok].bitcast(FP8X4),
@@ -197,15 +193,9 @@ def tile_hlgan_pb_t_kernel(tc, attn_l, wo_l, bo_l, g1, be1, wqkv_g, bqkv_g, out)
                         start=True,
                         stop=True,
                     )
-                    if c < 2:
-                        nc.vector.tensor_tensor(
-                            out=o_sb[g][:, q, cols], in0=acc[:], in1=bq_bc[:, cols], op=ALU.add
-                        )
-                    else:
-                        nc.scalar.copy(out=o_sb[g][:, q, cols], in_=acc[:])
-                        nc.gpsimd.tensor_tensor(
-                            out=o_sb[g][:, q, cols], in0=o_sb[g][:, q, cols], in1=bq_bc[:, cols], op=ALU.add
-                        )
+                    nc.vector.tensor_tensor(
+                        out=o_sb[g][:, q, cols], in0=acc[:], in1=bq_bc[:, cols], op=ALU.add
+                    )
                 if q == sizes[g] - 1:
                     nc.sync.dma_start(
                         out=out_dram[:, g * GROUP : g * GROUP + sizes[g], :], in_=o_sb[g][:, : sizes[g], :]

@@ -30,8 +30,9 @@ SQ_AT = 4
 RSTD_AT = 6
 Z_AT = 7
 ZT_AT = 9
-LQ_AT = 11
-OUT_AT = 12
+LG_AT = 10
+LQ_AT = 12
+OUT_AT = 13
 
 
 def transpose_rows(nc, banks, stage, ident, row_tiles):
@@ -82,8 +83,8 @@ def tile_hlgan_pb_t_kernel(tc, attn_l, wo_l, bo_l, g1, be1, wqkv_g, bqkv_g, out)
         scratch = ctx.enter_context(tc.tile_pool(name="scratch", bufs=4))
         l_pool = ctx.enter_context(tc.tile_pool(name="l", bufs=3))
         o_pool = ctx.enter_context(tc.tile_pool(name="o", bufs=4))
-        psum_v = ctx.enter_context(tc.psum_pool(name="psum_v", bufs=5))
-        psum_s = ctx.enter_context(tc.psum_pool(name="psum_s", bufs=3))
+        psum_v = ctx.enter_context(tc.psum_pool(name="psum_v", bufs=4))
+        psum_s = ctx.enter_context(tc.psum_pool(name="psum_s", bufs=4))
         ctx.enter_context(tc.manual_schedule())
 
         wo_sb = const.tile([P, 4, D], BF16)
@@ -139,8 +140,8 @@ def tile_hlgan_pb_t_kernel(tc, attn_l, wo_l, bo_l, g1, be1, wqkv_g, bqkv_g, out)
         gain_shift = const.tile([P, 2 * PACK], F32)
         nc.vector.tensor_copy(out=gain_shift[:], in_=gb_bank[:, 0:4].bitcast(BF16))
 
-        x_grouped, xq, xs, yb, ysum, ssq, rstd, nbias, lt, lq, ls, o_sb = (
-            {}, {}, {}, {}, {}, {}, {}, {}, {}, {}, {}, {},
+        x_grouped, xq, xs, yb, ysum, ssq, rstd, nbias, lt, lg, lq, ls, o_sb = (
+            {}, {}, {}, {}, {}, {}, {}, {}, {}, {}, {}, {}, {},
         )
 
         for step in range(GROUP * (n_groups - 1) + OUT_AT + GROUP):
@@ -156,23 +157,20 @@ def tile_hlgan_pb_t_kernel(tc, attn_l, wo_l, bo_l, g1, be1, wqkv_g, bqkv_g, out)
             g = group_at(step, LQ_AT)
             if g is not None:
                 toks = sizes[g] * P
-                lg = l_pool.tile([P, GROUP * P, PACK], BF16, align_bytes=64)
-                nc.vector.tensor_copy(
-                    out=lg[:, :toks, :], in_=lt[g][:, :, :toks].rearrange("p t c -> p c t")
-                )
                 lq[g] = q_pool.tile([P, GROUP * P], U32, align_bytes=64, name="lq")
                 ls[g] = q_pool.tile([P, GROUP * P], U8, align_bytes=64, name="ls")
                 nc.vector.quantize_mx(
                     out=lq[g][:, :toks].bitcast(FP8X4), scales=ls[g][:, :toks],
-                    in_=lg[:, :toks, :].rearrange("p c t -> p (c t)"),
+                    in_=lg[g][:, :toks, :].rearrange("p c t -> p (c t)"),
                 )
 
             gq = tile_at(step, Z_AT)
             if gq is not None:
                 g, q = gq
-                nc.scalar.activation(
-                    out=yb[g][:, q, :], in_=yb[g][:, q, :], func=ACT.Identity,
-                    bias=nbias[g][:, q : q + 1], scale=rstd[g][:, q : q + 1],
+                nc.gpsimd.tensor_scalar(
+                    out=yb[g][:, q, :], in0=yb[g][:, q, :],
+                    scalar1=rstd[g][:, q : q + 1], scalar2=nbias[g][:, q : q + 1],
+                    op0=ALU.mult, op1=ALU.add,
                 )
 
             gq = tile_at(step, OUT_AT)
@@ -183,7 +181,10 @@ def tile_hlgan_pb_t_kernel(tc, attn_l, wo_l, bo_l, g1, be1, wqkv_g, bqkv_g, out)
                 tok = slice(q * P, (q + 1) * P)
                 for c in range(3):
                     cols = slice(c * BANK, (c + 1) * BANK)
-                    acc = psum_v.tile([P, BANK], F32, tag="v")
+                    if c < 2:
+                        acc = psum_v.tile([P, BANK], F32, tag="v")
+                    else:
+                        acc = psum_s.tile([P, BANK], F32, tag="s")
                     nc.tensor.matmul_mx(
                         out=acc[:],
                         lhsT=lq[g][:, tok].bitcast(FP8X4),
@@ -193,9 +194,15 @@ def tile_hlgan_pb_t_kernel(tc, attn_l, wo_l, bo_l, g1, be1, wqkv_g, bqkv_g, out)
                         start=True,
                         stop=True,
                     )
-                    nc.vector.tensor_tensor(
-                        out=o_sb[g][:, q, cols], in0=acc[:], in1=bq_bc[:, cols], op=ALU.add
-                    )
+                    if c < 2:
+                        nc.vector.tensor_tensor(
+                            out=o_sb[g][:, q, cols], in0=acc[:], in1=bq_bc[:, cols], op=ALU.add
+                        )
+                    else:
+                        nc.scalar.copy(out=o_sb[g][:, q, cols], in_=acc[:])
+                        nc.gpsimd.tensor_tensor(
+                            out=o_sb[g][:, q, cols], in0=o_sb[g][:, q, cols], in1=bq_bc[:, cols], op=ALU.add
+                        )
                 if q == sizes[g] - 1:
                     nc.sync.dma_start(
                         out=out_dram[:, g * GROUP : g * GROUP + sizes[g], :], in_=o_sb[g][:, : sizes[g], :]
@@ -274,6 +281,15 @@ def tile_hlgan_pb_t_kernel(tc, attn_l, wo_l, bo_l, g1, be1, wqkv_g, bqkv_g, out)
                     nc.scalar.activation(
                         out=ssq[g][:, :n], in_=ssq[g][:, :n], func=ACT.Sqrt, bias=eps[:], scale=1.0 / D**3
                     )
+
+            g = group_at(step, LG_AT)
+            if g is not None:
+                toks = sizes[g] * P
+                lg[g] = l_pool.tile([P, GROUP * P, PACK], BF16, align_bytes=64, name="lg")
+                nc.scalar.copy(
+                    out=lg[g][:, :toks, :].rearrange("p (c i) t -> p c t i", i=4),
+                    in_=lt[g][:, :, :toks].rearrange("p t (c i) -> p c t i", i=4),
+                )
 
             g = group_at(step, RSTD_AT)
             if g is not None:

@@ -33,22 +33,23 @@ ZT_AT = 9
 LG_AT = 10
 LQ_AT = 12
 OUT_AT = 13
+WQ_AT = 7
 
 
-def transpose_rows(nc, banks, stage, ident, row_tiles):
+def transpose_rows(nc, banks, copy_out, stage, ident, row_tiles):
     n = len(row_tiles)
     grouped = stage.tile([P, n * P * PACK], BF16, align_bytes=64, tag="grouped")
     words = grouped[:].bitcast(F32).rearrange("p (r u) -> p r u", u=2)
     for first in range(0, n, 2):
         pair = row_tiles[first : first + 2]
         m = len(pair)
-        bank = banks.tile([P, 2, 2, P], F32, tag="s")
+        bank = banks.tile([P, 2, 2, P], F32, tag="bank")
         for r in range(m):
             for u in range(2):
                 nc.tensor.transpose(
                     out=bank[:, r, u, :], in_=pair[r][:, u * P : (u + 1) * P], identity=ident[:]
                 )
-        nc.scalar.copy(
+        copy_out(
             out=words[:, first * P : (first + m) * P, :].rearrange("p (r c) u -> p r c u", r=m),
             in_=bank[:, :m, :, :].rearrange("p r u c -> p r c u"),
         )
@@ -93,23 +94,23 @@ def tile_hlgan_pb_t_kernel(tc, attn_l, wo_l, bo_l, g1, be1, wqkv_g, bqkv_g, out)
                 out=wo_sb[:, 2 * u : 2 * u + 2, :],
                 in_=wo_l[256 * u : 256 * (u + 1), :].rearrange("(q e) k -> q e k", e=2),
             )
-        x_sb = []
+        gb_rows = const.tile([P, 2 * P], BF16)
+        nc.vector.memset(gb_rows[:], 0.0)
+        nc.sync.dma_start(out=gb_rows[0:2, :], in_=g1.rearrange("(u w) -> u w", u=2))
+        nc.sync.dma_start(out=gb_rows[2:4, :], in_=be1.rearrange("(u w) -> u w", u=2))
+        bo_bf = const.tile([P, D], BF16)
+        bq_bf = const.tile([P, D3], BF16)
         wqkv_sb = const.tile([P, D3 // P, D], BF16)
+        x_sb = []
         for g in range(n_groups):
             x_g = const.tile([P, sizes[g], D], BF16, name="x_%d" % g)
             nc.sync.dma_start(out=x_g[:], in_=x_dram[:, g * GROUP : g * GROUP + sizes[g], :])
             x_sb.append(x_g)
-            if g == 1:
+            if g == 0:
+                nc.sync.dma_start(out=bo_bf[:], in_=bo_l.partition_broadcast(P))
+            if g == 2:
                 nc.sync.dma_start(out=wqkv_sb[:], in_=wqkv_g.rearrange("(r q) k -> q r k", q=P))
-
-        bo_bf = const.tile([P, D], BF16)
-        nc.scalar.dma_start(out=bo_bf[:], in_=bo_l.partition_broadcast(P))
-        gb_rows = const.tile([P, 2 * P], BF16)
-        nc.vector.memset(gb_rows[:], 0.0)
-        nc.scalar.dma_start(out=gb_rows[0:2, :], in_=g1.rearrange("(u w) -> u w", u=2))
-        nc.scalar.dma_start(out=gb_rows[2:4, :], in_=be1.rearrange("(u w) -> u w", u=2))
-        bq_bf = const.tile([P, D3], BF16)
-        nc.scalar.dma_start(out=bq_bf[:], in_=bqkv_g.partition_broadcast(P))
+                nc.sync.dma_start(out=bq_bf[:], in_=bqkv_g.partition_broadcast(P))
 
         eps = const.tile([P, 1], F32)
         nc.vector.memset(eps[:], EPS)
@@ -121,7 +122,9 @@ def tile_hlgan_pb_t_kernel(tc, attn_l, wo_l, bo_l, g1, be1, wqkv_g, bqkv_g, out)
         wo_q = const.tile([P, D], U32, align_bytes=64)
         wo_s = const.tile([P, D], U8, align_bytes=64)
         wo_words = wo_sb[:].bitcast(F32)
-        wo_grouped = transpose_rows(nc, psum_s, stage, ident, [wo_words[:, r, :] for r in range(4)])
+        wo_grouped = transpose_rows(
+            nc, psum_v, nc.vector.tensor_copy, stage, ident, [wo_words[:, r, :] for r in range(4)]
+        )
         nc.vector.quantize_mx(out=wo_q[:].bitcast(FP8X4), scales=wo_s[:], in_=wo_grouped[:])
         wq_q = const.tile([P, D3], U32, align_bytes=64)
         wq_s = const.tile([P, D3], U8, align_bytes=64)
@@ -135,7 +138,7 @@ def tile_hlgan_pb_t_kernel(tc, attn_l, wo_l, bo_l, g1, be1, wqkv_g, bqkv_g, out)
         bq_bc = const.tile([P, D3], F32)
         nc.gpsimd.tensor_copy(out=bq_bc[:], in_=bq_bf[:])
 
-        gb_bank = psum_s.tile([P, P], F32, tag="s")
+        gb_bank = psum_v.tile([P, P], F32, tag="bank")
         nc.tensor.transpose(out=gb_bank[:], in_=gb_rows[:].bitcast(F32), identity=ident[:])
         gain_shift = const.tile([P, 2 * PACK], F32)
         nc.vector.tensor_copy(out=gain_shift[:], in_=gb_bank[:, 0:4].bitcast(BF16))
@@ -182,9 +185,9 @@ def tile_hlgan_pb_t_kernel(tc, attn_l, wo_l, bo_l, g1, be1, wqkv_g, bqkv_g, out)
                 for c in range(3):
                     cols = slice(c * BANK, (c + 1) * BANK)
                     if c < 2:
-                        acc = psum_v.tile([P, BANK], F32, tag="v")
+                        acc = psum_v.tile([P, BANK], F32, tag="bank")
                     else:
-                        acc = psum_s.tile([P, BANK], F32, tag="s")
+                        acc = psum_s.tile([P, BANK], F32, tag="bank")
                     nc.tensor.matmul_mx(
                         out=acc[:],
                         lhsT=lq[g][:, tok].bitcast(FP8X4),
@@ -214,7 +217,7 @@ def tile_hlgan_pb_t_kernel(tc, attn_l, wo_l, bo_l, g1, be1, wqkv_g, bqkv_g, out)
                 if q == 0:
                     yb[g] = y_pool.tile([P, GROUP, D], F32, name="yb")
                     ysum[g] = stat.tile([P, GROUP], F32, name="ysum")
-                y_ps = psum_v.tile([P, BANK], F32, tag="v")
+                y_ps = psum_v.tile([P, BANK], F32, tag="bank")
                 nc.tensor.matmul_mx(
                     out=y_ps[:],
                     lhsT=xq[g][:, q * P : (q + 1) * P].bitcast(FP8X4),
@@ -234,7 +237,7 @@ def tile_hlgan_pb_t_kernel(tc, attn_l, wo_l, bo_l, g1, be1, wqkv_g, bqkv_g, out)
                 n = sizes[g]
                 if h == 0:
                     lt[g] = l_pool.tile([P, PACK, GROUP * P], BF16, name="lt")
-                zt = psum_s.tile([P, 2, GROUP * P], F32, tag="s")
+                zt = psum_s.tile([P, 2, GROUP * P], F32, tag="bank")
                 for k in range(2):
                     t = 2 * h + k
                     for i in range(n):
@@ -253,14 +256,15 @@ def tile_hlgan_pb_t_kernel(tc, attn_l, wo_l, bo_l, g1, be1, wqkv_g, bqkv_g, out)
             if g is not None:
                 x_words = x_sb[g][:].bitcast(F32)
                 x_grouped[g] = transpose_rows(
-                    nc, psum_s, stage, ident, [x_words[:, i, :] for i in range(sizes[g])]
+                    nc, psum_s, nc.scalar.copy, stage, ident, [x_words[:, i, :] for i in range(sizes[g])]
                 )
 
-            if 1 <= step <= 3:
-                c = step - 1
+            if WQ_AT <= step < WQ_AT + 3:
+                c = step - WQ_AT
                 cols = slice(c * BANK, (c + 1) * BANK)
                 wq_grouped = transpose_rows(
-                    nc, psum_s, stage, ident, [wq_words[:, 4 * c + r, :] for r in range(4)]
+                    nc, psum_v, nc.vector.tensor_copy, stage, ident,
+                    [wq_words[:, 4 * c + r, :] for r in range(4)],
                 )
                 nc.vector.quantize_mx(
                     out=wq_q[:, cols].bitcast(FP8X4), scales=wq_s[:, cols], in_=wq_grouped[:]

@@ -23,17 +23,16 @@ EPS = 1e-5
 
 FLOPS = 2 * TOKENS * D * (D + D3)
 
-X_AT = 0
-XQ_AT = 2
-Y_AT = 3
-SQ_AT = 4
-RSTD_AT = 6
-Z_AT = 7
-ZT_AT = 9
-LG_AT = 10
-LQ_AT = 12
-OUT_AT = 13
-WQ_AT = 7
+X_LAG = 0
+XQ_LAG = 1
+Y_LAG = 2
+WQ_LAG = 3
+SQ_LAG = 3
+Z_LAG = 4
+L_LAG = 5
+OUT_LAG = 6
+STORE_LAG = 7
+GPSIMD_REGROUPS = 3
 
 
 def transpose_rows(nc, banks, copy_out, stage, ident, row_tiles):
@@ -63,22 +62,10 @@ def tile_hlgan_pb_t_kernel(tc, attn_l, wo_l, bo_l, g1, be1, wqkv_g, bqkv_g, out)
     sizes = [min(GROUP, TILES - j0) for j0 in range(0, TILES, GROUP)]
     n_groups = len(sizes)
 
-    def tile_at(step, lag):
-        g, q = divmod(step - lag, GROUP)
-        if 0 <= g < n_groups and q < sizes[g]:
-            return g, q
-        return None
-
-    def group_at(step, lag):
-        g, q = divmod(step - lag, GROUP)
-        if 0 <= g < n_groups and q == 0:
-            return g
-        return None
-
     with ExitStack() as ctx:
         const = ctx.enter_context(tc.tile_pool(name="const", bufs=1))
-        stage = ctx.enter_context(tc.tile_pool(name="stage", bufs=3))
-        q_pool = ctx.enter_context(tc.tile_pool(name="q", bufs=3))
+        stage = ctx.enter_context(tc.tile_pool(name="stage", bufs=4))
+        q_pool = ctx.enter_context(tc.tile_pool(name="q", bufs=4))
         y_pool = ctx.enter_context(tc.tile_pool(name="y", bufs=6))
         stat = ctx.enter_context(tc.tile_pool(name="stat", bufs=6))
         scratch = ctx.enter_context(tc.tile_pool(name="scratch", bufs=4))
@@ -108,8 +95,12 @@ def tile_hlgan_pb_t_kernel(tc, attn_l, wo_l, bo_l, g1, be1, wqkv_g, bqkv_g, out)
             x_sb.append(x_g)
             if g == 0:
                 nc.sync.dma_start(out=bo_bf[:], in_=bo_l.partition_broadcast(P))
-            if g == 2:
-                nc.sync.dma_start(out=wqkv_sb[:], in_=wqkv_g.rearrange("(r q) k -> q r k", q=P))
+            if g == 3:
+                for c in range(3):
+                    nc.sync.dma_start(
+                        out=wqkv_sb[:, 4 * c : 4 * c + 4, :],
+                        in_=wqkv_g[c * BANK : (c + 1) * BANK, :].rearrange("(r q) k -> q r k", q=P),
+                    )
                 nc.sync.dma_start(out=bq_bf[:], in_=bqkv_g.partition_broadcast(P))
 
         eps = const.tile([P, 1], F32)
@@ -143,80 +134,37 @@ def tile_hlgan_pb_t_kernel(tc, attn_l, wo_l, bo_l, g1, be1, wqkv_g, bqkv_g, out)
         gain_shift = const.tile([P, 2 * PACK], F32)
         nc.vector.tensor_copy(out=gain_shift[:], in_=gb_bank[:, 0:4].bitcast(BF16))
 
-        x_grouped, xq, xs, yb, ysum, ssq, rstd, nbias, lt, lg, lq, ls, o_sb = (
-            {}, {}, {}, {}, {}, {}, {}, {}, {}, {}, {}, {}, {},
+        x_grouped, xq, xs, yb, ysum, mean, ssq, rstd, zt, lt, lg, lq, ls, o_sb = (
+            {}, {}, {}, {}, {}, {}, {}, {}, {}, {}, {}, {}, {}, {},
         )
 
-        for step in range(GROUP * (n_groups - 1) + OUT_AT + GROUP):
-            g = group_at(step, XQ_AT)
-            if g is not None:
-                toks = sizes[g] * P
-                xq[g] = q_pool.tile([P, GROUP * P], U32, align_bytes=64, name="xq")
-                xs[g] = q_pool.tile([P, GROUP * P], U8, align_bytes=64, name="xs")
-                nc.vector.quantize_mx(
-                    out=xq[g][:, :toks].bitcast(FP8X4), scales=xs[g][:, :toks], in_=x_grouped[g][:]
-                )
+        def transpose_x(g):
+            x_words = x_sb[g][:].bitcast(F32)
+            x_grouped[g] = transpose_rows(
+                nc, psum_s, nc.scalar.copy, stage, ident, [x_words[:, i, :] for i in range(sizes[g])]
+            )
 
-            g = group_at(step, LQ_AT)
-            if g is not None:
-                toks = sizes[g] * P
-                lq[g] = q_pool.tile([P, GROUP * P], U32, align_bytes=64, name="lq")
-                ls[g] = q_pool.tile([P, GROUP * P], U8, align_bytes=64, name="ls")
-                nc.vector.quantize_mx(
-                    out=lq[g][:, :toks].bitcast(FP8X4), scales=ls[g][:, :toks],
-                    in_=lg[g][:, :toks, :].rearrange("p c t -> p (c t)"),
-                )
+        def quantize_x(g):
+            toks = sizes[g] * P
+            xq[g] = q_pool.tile([P, GROUP * P], U32, align_bytes=64, name="xq")
+            xs[g] = q_pool.tile([P, GROUP * P], U8, align_bytes=64, name="xs")
+            nc.vector.quantize_mx(
+                out=xq[g][:, :toks].bitcast(FP8X4), scales=xs[g][:, :toks], in_=x_grouped[g][:]
+            )
 
-            gq = tile_at(step, Z_AT)
-            if gq is not None:
-                g, q = gq
-                nc.gpsimd.tensor_scalar(
-                    out=yb[g][:, q, :], in0=yb[g][:, q, :],
-                    scalar1=rstd[g][:, q : q + 1], scalar2=nbias[g][:, q : q + 1],
-                    op0=ALU.mult, op1=ALU.add,
-                )
+        def quantize_local(g):
+            toks = sizes[g] * P
+            lq[g] = q_pool.tile([P, GROUP * P], U32, align_bytes=64, name="lq")
+            ls[g] = q_pool.tile([P, GROUP * P], U8, align_bytes=64, name="ls")
+            nc.vector.quantize_mx(
+                out=lq[g][:, :toks].bitcast(FP8X4), scales=ls[g][:, :toks],
+                in_=lg[g][:, :toks, :].rearrange("p c t -> p (c t)"),
+            )
 
-            gq = tile_at(step, OUT_AT)
-            if gq is not None:
-                g, q = gq
-                if q == 0:
-                    o_sb[g] = o_pool.tile([P, GROUP, D3], F32, name="o_sb")
-                tok = slice(q * P, (q + 1) * P)
-                for c in range(3):
-                    cols = slice(c * BANK, (c + 1) * BANK)
-                    if c < 2:
-                        acc = psum_v.tile([P, BANK], F32, tag="bank")
-                    else:
-                        acc = psum_s.tile([P, BANK], F32, tag="bank")
-                    nc.tensor.matmul_mx(
-                        out=acc[:],
-                        lhsT=lq[g][:, tok].bitcast(FP8X4),
-                        lhsT_scale=ls[g][:, tok],
-                        rhs=wq_q[:, cols].bitcast(FP8X4),
-                        rhs_scale=wq_s[:, cols],
-                        start=True,
-                        stop=True,
-                    )
-                    if c < 2:
-                        nc.vector.tensor_tensor(
-                            out=o_sb[g][:, q, cols], in0=acc[:], in1=bq_bc[:, cols], op=ALU.add
-                        )
-                    else:
-                        nc.scalar.copy(out=o_sb[g][:, q, cols], in_=acc[:])
-                        nc.gpsimd.tensor_tensor(
-                            out=o_sb[g][:, q, cols], in0=o_sb[g][:, q, cols], in1=bq_bc[:, cols], op=ALU.add
-                        )
-                if q == sizes[g] - 1:
-                    nc.sync.dma_start(
-                        out=out_dram[:, g * GROUP : g * GROUP + sizes[g], :], in_=o_sb[g][:, : sizes[g], :]
-                    )
-
-            gq = tile_at(step, Y_AT)
-            if gq is not None:
-                g, q = gq
-                if q == 0:
-                    yb[g] = y_pool.tile([P, GROUP, D], F32, name="yb")
-                    ysum[g] = stat.tile([P, GROUP], F32, name="ysum")
+        def first_product(g):
+            yb[g] = y_pool.tile([P, GROUP, D], F32, name="yb")
+            ysum[g] = stat.tile([P, GROUP], F32, name="ysum")
+            for q in range(sizes[g]):
                 y_ps = psum_v.tile([P, BANK], F32, tag="bank")
                 nc.tensor.matmul_mx(
                     out=y_ps[:],
@@ -232,76 +180,148 @@ def tile_hlgan_pb_t_kernel(tc, attn_l, wo_l, bo_l, g1, be1, wqkv_g, bqkv_g, out)
                     op0=ALU.mult, op1=ALU.add, accum_out=ysum[g][:, q : q + 1],
                 )
 
-            g, h = divmod(step - ZT_AT, GROUP)
-            if 0 <= g < n_groups:
-                n = sizes[g]
-                if h == 0:
-                    lt[g] = l_pool.tile([P, PACK, GROUP * P], BF16, name="lt")
-                zt = psum_s.tile([P, 2, GROUP * P], F32, tag="bank")
-                for k in range(2):
-                    t = 2 * h + k
-                    for i in range(n):
-                        nc.tensor.transpose(
-                            out=zt[:, k, i * P : (i + 1) * P], in_=yb[g][:, i, t * P : (t + 1) * P],
-                            identity=ident[:],
-                        )
-                for k in range(2):
-                    t = 2 * h + k
-                    nc.scalar.activation(
-                        out=lt[g][:, t, : n * P], in_=zt[:, k, : n * P], func=ACT.Identity,
-                        bias=gain_shift[:, PACK + t : PACK + t + 1], scale=gain_shift[:, t : t + 1],
-                    )
+        def row_means(g):
+            n = sizes[g]
+            mean[g] = stat.tile([P, GROUP], F32, name="mean")
+            nc.scalar.activation(out=mean[g][:, :n], in_=ysum[g][:, :n], func=ACT.Copy, scale=1.0 / D)
 
-            g = group_at(step, X_AT)
-            if g is not None:
-                x_words = x_sb[g][:].bitcast(F32)
-                x_grouped[g] = transpose_rows(
-                    nc, psum_s, nc.scalar.copy, stage, ident, [x_words[:, i, :] for i in range(sizes[g])]
-                )
-
-            if WQ_AT <= step < WQ_AT + 3:
-                c = step - WQ_AT
-                cols = slice(c * BANK, (c + 1) * BANK)
-                wq_grouped = transpose_rows(
-                    nc, psum_v, nc.vector.tensor_copy, stage, ident,
-                    [wq_words[:, 4 * c + r, :] for r in range(4)],
-                )
-                nc.vector.quantize_mx(
-                    out=wq_q[:, cols].bitcast(FP8X4), scales=wq_s[:, cols], in_=wq_grouped[:]
-                )
-
-            gq = tile_at(step, SQ_AT)
-            if gq is not None:
-                g, q = gq
-                if q == 0:
-                    ssq[g] = stat.tile([P, GROUP], F32, name="ssq")
-                sq = scratch.tile([P, D], BF16)
+        def row_stds(g):
+            n = sizes[g]
+            ssq[g] = stat.tile([P, GROUP], F32, name="ssq")
+            for q in range(n):
+                sq = scratch.tile([P, D], BF16, name="sq")
                 nc.scalar.activation(
                     out=sq[:], in_=yb[g][:, q, :], func=ACT.Square,
-                    bias=ysum[g][:, q : q + 1], scale=-float(D), accum_out=ssq[g][:, q : q + 1],
+                    bias=mean[g][:, q : q + 1], scale=-1.0, accum_out=ssq[g][:, q : q + 1],
                 )
-                if q == sizes[g] - 1:
-                    n = sizes[g]
-                    nc.scalar.activation(
-                        out=ssq[g][:, :n], in_=ssq[g][:, :n], func=ACT.Sqrt, bias=eps[:], scale=1.0 / D**3
-                    )
+            nc.scalar.activation(
+                out=ssq[g][:, :n], in_=ssq[g][:, :n], func=ACT.Sqrt, bias=eps[:], scale=1.0 / D
+            )
 
-            g = group_at(step, LG_AT)
-            if g is not None:
-                toks = sizes[g] * P
-                lg[g] = l_pool.tile([P, GROUP * P, PACK], BF16, align_bytes=64, name="lg")
-                nc.scalar.copy(
-                    out=lg[g][:, :toks, :].rearrange("p (c i) t -> p c t i", i=4),
-                    in_=lt[g][:, :, :toks].rearrange("p t (c i) -> p c t i", i=4),
+        def reciprocal_stds(g):
+            n = sizes[g]
+            rstd[g] = stat.tile([P, GROUP], F32, name="rstd")
+            nc.vector.reciprocal(rstd[g][:, :n], ssq[g][:, :n])
+
+        def normalise(g):
+            for q in range(sizes[g]):
+                nc.gpsimd.tensor_scalar(
+                    out=yb[g][:, q, :], in0=yb[g][:, q, :],
+                    scalar1=mean[g][:, q : q + 1], scalar2=rstd[g][:, q : q + 1],
+                    op0=ALU.subtract, op1=ALU.mult,
                 )
 
-            g = group_at(step, RSTD_AT)
-            if g is not None:
-                n = sizes[g]
-                rstd[g] = stat.tile([P, GROUP], F32, name="rstd")
-                nc.vector.reciprocal(rstd[g][:, :n], ssq[g][:, :n])
-                nbias[g] = stat.tile([P, GROUP], F32, name="nbias")
-                nc.vector.scalar_tensor_tensor(
-                    out=nbias[g][:, :n], in0=ysum[g][:, :n], scalar=-1.0 / D, in1=rstd[g][:, :n],
-                    op0=ALU.mult, op1=ALU.mult,
+        def transpose_z(g):
+            for h in range(2):
+                bank = psum_s.tile([P, 2, GROUP * P], F32, tag="bank")
+                zt[g, h] = bank
+                for k in range(2):
+                    t = 2 * h + k
+                    for i in range(sizes[g]):
+                        nc.tensor.transpose(
+                            out=bank[:, k, i * P : (i + 1) * P], in_=yb[g][:, i, t * P : (t + 1) * P],
+                            identity=ident[:],
+                        )
+
+        def gain_and_shift(g):
+            toks = sizes[g] * P
+            lt[g] = l_pool.tile([P, PACK, GROUP * P], BF16, name="lt")
+            for t in range(PACK):
+                nc.scalar.activation(
+                    out=lt[g][:, t, :toks], in_=zt[g, t // 2][:, t % 2, :toks], func=ACT.Identity,
+                    bias=gain_shift[:, PACK + t : PACK + t + 1], scale=gain_shift[:, t : t + 1],
                 )
+
+        def regroup(g):
+            toks = sizes[g] * P
+            lg[g] = l_pool.tile([P, GROUP * P, PACK], BF16, align_bytes=64, name="lg")
+            side_by_side = lg[g][:, :toks, :].rearrange("p (c i) t -> p c t i", i=4)
+            apart = lt[g][:, :, :toks].rearrange("p t (c i) -> p c t i", i=4)
+            if g % GPSIMD_REGROUPS == 0:
+                nc.gpsimd.tensor_scalar(
+                    out=side_by_side, in0=apart, scalar1=1.0, scalar2=0.0, op0=ALU.mult, op1=ALU.add
+                )
+            else:
+                nc.scalar.copy(out=side_by_side, in_=apart)
+
+        def second_product(g, q, c, banks):
+            tok = slice(q * P, (q + 1) * P)
+            cols = slice(c * BANK, (c + 1) * BANK)
+            acc = banks.tile([P, BANK], F32, tag="bank")
+            nc.tensor.matmul_mx(
+                out=acc[:],
+                lhsT=lq[g][:, tok].bitcast(FP8X4),
+                lhsT_scale=ls[g][:, tok],
+                rhs=wq_q[:, cols].bitcast(FP8X4),
+                rhs_scale=wq_s[:, cols],
+                start=True,
+                stop=True,
+            )
+            return acc
+
+        def out_by_vector(g, q, c):
+            cols = slice(c * BANK, (c + 1) * BANK)
+            acc = second_product(g, q, c, psum_v)
+            nc.vector.tensor_tensor(out=o_sb[g][:, q, cols], in0=acc[:], in1=bq_bc[:, cols], op=ALU.add)
+
+        def out_by_scalar(g, q, c):
+            cols = slice(c * BANK, (c + 1) * BANK)
+            acc = second_product(g, q, c, psum_s)
+            nc.scalar.copy(out=o_sb[g][:, q, cols], in_=acc[:])
+
+        def store(g):
+            cols = slice(2 * BANK, 3 * BANK)
+            nc.gpsimd.tensor_tensor(
+                out=o_sb[g][:, 0, cols], in0=o_sb[g][:, 0, cols], in1=bq_bc[:, cols], op=ALU.add
+            )
+            nc.sync.dma_start(
+                out=out_dram[:, g * GROUP : g * GROUP + sizes[g], :], in_=o_sb[g][:, : sizes[g], :]
+            )
+
+        def pack_wqkv(c):
+            cols = slice(c * BANK, (c + 1) * BANK)
+            wq_grouped = transpose_rows(
+                nc, psum_v, nc.vector.tensor_copy, stage, ident, [wq_words[:, 4 * c + r, :] for r in range(4)]
+            )
+            nc.vector.quantize_mx(out=wq_q[:, cols].bitcast(FP8X4), scales=wq_s[:, cols], in_=wq_grouped[:])
+
+        for period in range(n_groups + STORE_LAG):
+
+            def due(lag):
+                return [period - lag] if 0 <= period - lag < n_groups else []
+
+            for g in due(X_LAG):
+                transpose_x(g)
+            for g in due(XQ_LAG):
+                quantize_x(g)
+            for g in due(Z_LAG):
+                reciprocal_stds(g)
+            for g in due(OUT_LAG):
+                quantize_local(g)
+            for g in due(Z_LAG):
+                normalise(g)
+            for g in due(Y_LAG):
+                first_product(g)
+            if WQ_LAG <= period < WQ_LAG + 3:
+                pack_wqkv(period - WQ_LAG)
+            for g in due(L_LAG):
+                gain_and_shift(g)
+            for g in due(SQ_LAG):
+                row_stds(g)
+            for g in due(Y_LAG):
+                row_means(g)
+            for g in due(STORE_LAG):
+                store(g)
+            for g in due(OUT_LAG):
+                o_sb[g] = o_pool.tile([P, GROUP, D3], F32, name="o_sb")
+                for q in range(sizes[g]):
+                    for c in range(2):
+                        out_by_vector(g, q, c)
+            for g in due(L_LAG):
+                regroup(g)
+            for g in due(OUT_LAG):
+                out_by_scalar(g, 0, 2)
+                if sizes[g] == 2:
+                    out_by_vector(g, 1, 2)
+            for g in due(Z_LAG):
+                transpose_z(g)

@@ -134,8 +134,8 @@ def tile_hlgan_pb_t_kernel(tc, attn_l, wo_l, bo_l, g1, be1, wqkv_g, bqkv_g, out)
         gain_shift = const.tile([P, 2 * PACK], F32)
         nc.vector.tensor_copy(out=gain_shift[:], in_=gb_bank[:, 0:4].bitcast(BF16))
 
-        x_grouped, xq, xs, yb, ysum, mean, ssq, rstd, zt, lt, lg, lq, ls, o_sb = (
-            {}, {}, {}, {}, {}, {}, {}, {}, {}, {}, {}, {}, {}, {},
+        x_grouped, xq, xs, yb, ysum, neg_mean, ssq, rstd, nbias, zt, lt, lg, lq, ls, o_sb = (
+            {}, {}, {}, {}, {}, {}, {}, {}, {}, {}, {}, {}, {}, {}, {},
         )
 
         def transpose_x(g):
@@ -182,8 +182,8 @@ def tile_hlgan_pb_t_kernel(tc, attn_l, wo_l, bo_l, g1, be1, wqkv_g, bqkv_g, out)
 
         def row_means(g):
             n = sizes[g]
-            mean[g] = stat.tile([P, GROUP], F32, name="mean")
-            nc.scalar.activation(out=mean[g][:, :n], in_=ysum[g][:, :n], func=ACT.Copy, scale=1.0 / D)
+            neg_mean[g] = stat.tile([P, GROUP], F32, name="neg_mean")
+            nc.scalar.activation(out=neg_mean[g][:, :n], in_=ysum[g][:, :n], func=ACT.Copy, scale=-1.0 / D)
 
         def row_stds(g):
             n = sizes[g]
@@ -192,7 +192,7 @@ def tile_hlgan_pb_t_kernel(tc, attn_l, wo_l, bo_l, g1, be1, wqkv_g, bqkv_g, out)
                 sq = scratch.tile([P, D], BF16, name="sq")
                 nc.scalar.activation(
                     out=sq[:], in_=yb[g][:, q, :], func=ACT.Square,
-                    bias=mean[g][:, q : q + 1], scale=-1.0, accum_out=ssq[g][:, q : q + 1],
+                    bias=neg_mean[g][:, q : q + 1], scale=1.0, accum_out=ssq[g][:, q : q + 1],
                 )
             nc.scalar.activation(
                 out=ssq[g][:, :n], in_=ssq[g][:, :n], func=ACT.Sqrt, bias=eps[:], scale=1.0 / D
@@ -203,12 +203,19 @@ def tile_hlgan_pb_t_kernel(tc, attn_l, wo_l, bo_l, g1, be1, wqkv_g, bqkv_g, out)
             rstd[g] = stat.tile([P, GROUP], F32, name="rstd")
             nc.vector.reciprocal(rstd[g][:, :n], ssq[g][:, :n])
 
+        def scaled_means(g):
+            n = sizes[g]
+            nbias[g] = stat.tile([P, GROUP], F32, name="nbias")
+            nc.vector.tensor_tensor(
+                out=nbias[g][:, :n], in0=neg_mean[g][:, :n], in1=rstd[g][:, :n], op=ALU.mult
+            )
+
         def normalise(g):
             for q in range(sizes[g]):
                 nc.gpsimd.tensor_scalar(
                     out=yb[g][:, q, :], in0=yb[g][:, q, :],
-                    scalar1=mean[g][:, q : q + 1], scalar2=rstd[g][:, q : q + 1],
-                    op0=ALU.subtract, op1=ALU.mult,
+                    scalar1=rstd[g][:, q : q + 1], scalar2=nbias[g][:, q : q + 1],
+                    op0=ALU.mult, op1=ALU.add,
                 )
 
         def transpose_z(g):
@@ -235,14 +242,16 @@ def tile_hlgan_pb_t_kernel(tc, attn_l, wo_l, bo_l, g1, be1, wqkv_g, bqkv_g, out)
         def regroup(g):
             toks = sizes[g] * P
             lg[g] = l_pool.tile([P, GROUP * P, PACK], BF16, align_bytes=64, name="lg")
-            side_by_side = lg[g][:, :toks, :].rearrange("p (c i) t -> p c t i", i=4)
-            apart = lt[g][:, :, :toks].rearrange("p t (c i) -> p c t i", i=4)
             if g % GPSIMD_REGROUPS == 0:
                 nc.gpsimd.tensor_scalar(
-                    out=side_by_side, in0=apart, scalar1=1.0, scalar2=0.0, op0=ALU.mult, op1=ALU.add
+                    out=lg[g][:, :toks, :], in0=lt[g][:, :, :toks].rearrange("p t c -> p c t"),
+                    scalar1=1.0, scalar2=0.0, op0=ALU.mult, op1=ALU.add,
                 )
             else:
-                nc.scalar.copy(out=side_by_side, in_=apart)
+                nc.scalar.copy(
+                    out=lg[g][:, :toks, :].rearrange("p (c i) t -> p c t i", i=4),
+                    in_=lt[g][:, :, :toks].rearrange("p t (c i) -> p c t i", i=4),
+                )
 
         def second_product(g, q, c, banks):
             tok = slice(q * P, (q + 1) * P)
@@ -292,10 +301,12 @@ def tile_hlgan_pb_t_kernel(tc, attn_l, wo_l, bo_l, g1, be1, wqkv_g, bqkv_g, out)
 
             for g in due(X_LAG):
                 transpose_x(g)
+            for g in due(Z_LAG):
+                reciprocal_stds(g)
             for g in due(XQ_LAG):
                 quantize_x(g)
             for g in due(Z_LAG):
-                reciprocal_stds(g)
+                scaled_means(g)
             for g in due(OUT_LAG):
                 quantize_local(g)
             for g in due(Z_LAG):

@@ -32,7 +32,6 @@ Z_LAG = 4
 L_LAG = 5
 OUT_LAG = 6
 STORE_LAG = 7
-GPSIMD_REGROUPS = 3
 
 
 def transpose_rows(nc, banks, copy_out, stage, ident, row_tiles):
@@ -106,7 +105,7 @@ def tile_hlgan_pb_t_kernel(tc, attn_l, wo_l, bo_l, g1, be1, wqkv_g, bqkv_g, out)
         eps = const.tile([P, 1], F32)
         nc.vector.memset(eps[:], EPS)
         warm = const.tile([P, 1], F32)
-        nc.scalar.activation(out=warm[:], in_=eps[:], func=ACT.Sqrt)
+        nc.scalar.activation(out=warm[:], in_=eps[:], func=ACT.Abs_reciprocal_sqrt)
         ident = const.tile([P, P], F32)
         make_identity(nc, ident[:])
 
@@ -134,8 +133,8 @@ def tile_hlgan_pb_t_kernel(tc, attn_l, wo_l, bo_l, g1, be1, wqkv_g, bqkv_g, out)
         gain_shift = const.tile([P, 2 * PACK], F32)
         nc.vector.tensor_copy(out=gain_shift[:], in_=gb_bank[:, 0:4].bitcast(BF16))
 
-        x_grouped, xq, xs, yb, ysum, neg_mean, ssq, rstd, nbias, zt, lt, lg, lq, ls, o_sb = (
-            {}, {}, {}, {}, {}, {}, {}, {}, {}, {}, {}, {}, {}, {}, {},
+        x_grouped, xq, xs, yb, ysum, ssq, rstd, nbias, zt, lt, lg, lq, ls, o_sb = (
+            {}, {}, {}, {}, {}, {}, {}, {}, {}, {}, {}, {}, {}, {},
         )
 
         def transpose_x(g):
@@ -180,34 +179,26 @@ def tile_hlgan_pb_t_kernel(tc, attn_l, wo_l, bo_l, g1, be1, wqkv_g, bqkv_g, out)
                     op0=ALU.mult, op1=ALU.add, accum_out=ysum[g][:, q : q + 1],
                 )
 
-        def row_means(g):
-            n = sizes[g]
-            neg_mean[g] = stat.tile([P, GROUP], F32, name="neg_mean")
-            nc.scalar.activation(out=neg_mean[g][:, :n], in_=ysum[g][:, :n], func=ACT.Copy, scale=-1.0 / D)
-
         def row_stds(g):
             n = sizes[g]
+            rstd[g] = stat.tile([P, GROUP], F32, name="rstd")
             ssq[g] = stat.tile([P, GROUP], F32, name="ssq")
             for q in range(n):
                 sq = scratch.tile([P, D], BF16, name="sq")
                 nc.scalar.activation(
                     out=sq[:], in_=yb[g][:, q, :], func=ACT.Square,
-                    bias=neg_mean[g][:, q : q + 1], scale=1.0, accum_out=ssq[g][:, q : q + 1],
+                    bias=ysum[g][:, q : q + 1], scale=-float(D), accum_out=ssq[g][:, q : q + 1],
                 )
             nc.scalar.activation(
-                out=ssq[g][:, :n], in_=ssq[g][:, :n], func=ACT.Sqrt, bias=eps[:], scale=1.0 / D
+                out=rstd[g][:, :n], in_=ssq[g][:, :n], func=ACT.Abs_reciprocal_sqrt, bias=eps[:], scale=1.0 / D**3
             )
-
-        def reciprocal_stds(g):
-            n = sizes[g]
-            rstd[g] = stat.tile([P, GROUP], F32, name="rstd")
-            nc.vector.reciprocal(rstd[g][:, :n], ssq[g][:, :n])
 
         def scaled_means(g):
             n = sizes[g]
             nbias[g] = stat.tile([P, GROUP], F32, name="nbias")
-            nc.vector.tensor_tensor(
-                out=nbias[g][:, :n], in0=neg_mean[g][:, :n], in1=rstd[g][:, :n], op=ALU.mult
+            nc.vector.scalar_tensor_tensor(
+                out=nbias[g][:, :n], in0=ysum[g][:, :n], scalar=-1.0 / D, in1=rstd[g][:, :n],
+                op0=ALU.mult, op1=ALU.mult,
             )
 
         def normalise(g):
@@ -242,16 +233,10 @@ def tile_hlgan_pb_t_kernel(tc, attn_l, wo_l, bo_l, g1, be1, wqkv_g, bqkv_g, out)
         def regroup(g):
             toks = sizes[g] * P
             lg[g] = l_pool.tile([P, GROUP * P, PACK], BF16, align_bytes=64, name="lg")
-            if g % GPSIMD_REGROUPS == 0:
-                nc.gpsimd.tensor_scalar(
-                    out=lg[g][:, :toks, :], in0=lt[g][:, :, :toks].rearrange("p t c -> p c t"),
-                    scalar1=1.0, scalar2=0.0, op0=ALU.mult, op1=ALU.add,
-                )
-            else:
-                nc.scalar.copy(
-                    out=lg[g][:, :toks, :].rearrange("p (c i) t -> p c t i", i=4),
-                    in_=lt[g][:, :, :toks].rearrange("p t (c i) -> p c t i", i=4),
-                )
+            nc.scalar.copy(
+                out=lg[g][:, :toks, :].rearrange("p (c i) t -> p c t i", i=4),
+                in_=lt[g][:, :, :toks].rearrange("p t (c i) -> p c t i", i=4),
+            )
 
         def second_product(g, q, c, banks):
             tok = slice(q * P, (q + 1) * P)
@@ -278,14 +263,15 @@ def tile_hlgan_pb_t_kernel(tc, attn_l, wo_l, bo_l, g1, be1, wqkv_g, bqkv_g, out)
             acc = second_product(g, q, c, psum_s)
             nc.scalar.copy(out=o_sb[g][:, q, cols], in_=acc[:])
 
-        def store(g):
+        def store(g, q):
+            nc.sync.dma_start(out=out_dram[:, g * GROUP + q, :], in_=o_sb[g][:, q, :])
+
+        def finish_first_tile(g):
             cols = slice(2 * BANK, 3 * BANK)
             nc.gpsimd.tensor_tensor(
                 out=o_sb[g][:, 0, cols], in0=o_sb[g][:, 0, cols], in1=bq_bc[:, cols], op=ALU.add
             )
-            nc.sync.dma_start(
-                out=out_dram[:, g * GROUP : g * GROUP + sizes[g], :], in_=o_sb[g][:, : sizes[g], :]
-            )
+            store(g, 0)
 
         def pack_wqkv(c):
             cols = slice(c * BANK, (c + 1) * BANK)
@@ -301,14 +287,17 @@ def tile_hlgan_pb_t_kernel(tc, attn_l, wo_l, bo_l, g1, be1, wqkv_g, bqkv_g, out)
 
             for g in due(X_LAG):
                 transpose_x(g)
-            for g in due(Z_LAG):
-                reciprocal_stds(g)
             for g in due(XQ_LAG):
                 quantize_x(g)
             for g in due(Z_LAG):
                 scaled_means(g)
             for g in due(OUT_LAG):
                 quantize_local(g)
+            for g in due(STORE_LAG):
+                if sizes[g] == 2:
+                    out_by_vector(g, 1, 1)
+                    out_by_vector(g, 1, 2)
+                    store(g, 1)
             for g in due(Z_LAG):
                 normalise(g)
             for g in due(Y_LAG):
@@ -319,20 +308,17 @@ def tile_hlgan_pb_t_kernel(tc, attn_l, wo_l, bo_l, g1, be1, wqkv_g, bqkv_g, out)
                 gain_and_shift(g)
             for g in due(SQ_LAG):
                 row_stds(g)
-            for g in due(Y_LAG):
-                row_means(g)
             for g in due(STORE_LAG):
-                store(g)
+                finish_first_tile(g)
             for g in due(OUT_LAG):
                 o_sb[g] = o_pool.tile([P, GROUP, D3], F32, name="o_sb")
-                for q in range(sizes[g]):
-                    for c in range(2):
-                        out_by_vector(g, q, c)
+                out_by_vector(g, 0, 0)
+                out_by_vector(g, 0, 1)
+                if sizes[g] == 2:
+                    out_by_vector(g, 1, 0)
             for g in due(L_LAG):
                 regroup(g)
             for g in due(OUT_LAG):
                 out_by_scalar(g, 0, 2)
-                if sizes[g] == 2:
-                    out_by_vector(g, 1, 2)
             for g in due(Z_LAG):
                 transpose_z(g)

@@ -180,15 +180,17 @@ def tile_hlgan_pb_t_kernel(tc, attn_l, wo_l, bo_l, g1, be1, wqkv_g, bqkv_g, out)
                 )
 
         def row_stds(g):
-            n = sizes[g]
-            rstd[g] = stat.tile([P, GROUP], F32, name="rstd")
             ssq[g] = stat.tile([P, GROUP], F32, name="ssq")
-            for q in range(n):
+            for q in range(sizes[g]):
                 sq = scratch.tile([P, D], BF16, name="sq")
                 nc.scalar.activation(
                     out=sq[:], in_=yb[g][:, q, :], func=ACT.Square,
                     bias=ysum[g][:, q : q + 1], scale=-float(D), accum_out=ssq[g][:, q : q + 1],
                 )
+
+        def reciprocal_stds(g):
+            n = sizes[g]
+            rstd[g] = stat.tile([P, GROUP], F32, name="rstd")
             nc.scalar.activation(
                 out=rstd[g][:, :n], in_=ssq[g][:, :n], func=ACT.Abs_reciprocal_sqrt, bias=eps[:], scale=1.0 / D**3
             )
@@ -233,6 +235,12 @@ def tile_hlgan_pb_t_kernel(tc, attn_l, wo_l, bo_l, g1, be1, wqkv_g, bqkv_g, out)
         def regroup(g):
             toks = sizes[g] * P
             lg[g] = l_pool.tile([P, GROUP * P, PACK], BF16, align_bytes=64, name="lg")
+            if g % 3 == 1:
+                nc.gpsimd.tensor_scalar(
+                    out=lg[g][:, :toks, :], in0=lt[g][:, :, :toks].rearrange("p t c -> p c t"),
+                    scalar1=1.0, scalar2=0.0, op0=ALU.mult, op1=ALU.add,
+                )
+                return
             nc.scalar.copy(
                 out=lg[g][:, :toks, :].rearrange("p (c i) t -> p c t i", i=4),
                 in_=lt[g][:, :, :toks].rearrange("p t (c i) -> p c t i", i=4),
@@ -257,21 +265,23 @@ def tile_hlgan_pb_t_kernel(tc, attn_l, wo_l, bo_l, g1, be1, wqkv_g, bqkv_g, out)
             cols = slice(c * BANK, (c + 1) * BANK)
             acc = second_product(g, q, c, psum_v)
             nc.vector.tensor_tensor(out=o_sb[g][:, q, cols], in0=acc[:], in1=bq_bc[:, cols], op=ALU.add)
+            if g >= n_groups - 2:
+                store(g, q, cols)
 
         def out_by_scalar(g, q, c):
             cols = slice(c * BANK, (c + 1) * BANK)
             acc = second_product(g, q, c, psum_s)
             nc.scalar.copy(out=o_sb[g][:, q, cols], in_=acc[:])
 
-        def store(g, q):
-            nc.sync.dma_start(out=out_dram[:, g * GROUP + q, :], in_=o_sb[g][:, q, :])
+        def store(g, q, cols):
+            nc.sync.dma_start(out=out_dram[:, g * GROUP + q, cols], in_=o_sb[g][:, q, cols])
 
         def finish_first_tile(g):
             cols = slice(2 * BANK, 3 * BANK)
             nc.gpsimd.tensor_tensor(
                 out=o_sb[g][:, 0, cols], in0=o_sb[g][:, 0, cols], in1=bq_bc[:, cols], op=ALU.add
             )
-            store(g, 0)
+            store(g, 0, cols if g >= n_groups - 2 else slice(0, D3))
 
         def pack_wqkv(c):
             cols = slice(c * BANK, (c + 1) * BANK)
@@ -297,7 +307,8 @@ def tile_hlgan_pb_t_kernel(tc, attn_l, wo_l, bo_l, g1, be1, wqkv_g, bqkv_g, out)
                 if sizes[g] == 2:
                     out_by_vector(g, 1, 1)
                     out_by_vector(g, 1, 2)
-                    store(g, 1)
+                    if g < n_groups - 2:
+                        store(g, 1, slice(0, D3))
             for g in due(Z_LAG):
                 normalise(g)
             for g in due(Y_LAG):
@@ -318,6 +329,8 @@ def tile_hlgan_pb_t_kernel(tc, attn_l, wo_l, bo_l, g1, be1, wqkv_g, bqkv_g, out)
                     out_by_vector(g, 1, 0)
             for g in due(L_LAG):
                 regroup(g)
+            for g in due(SQ_LAG):
+                reciprocal_stds(g)
             for g in due(OUT_LAG):
                 out_by_scalar(g, 0, 2)
             for g in due(Z_LAG):

@@ -235,12 +235,6 @@ def tile_hlgan_pb_t_kernel(tc, attn_l, wo_l, bo_l, g1, be1, wqkv_g, bqkv_g, out)
         def regroup(g):
             toks = sizes[g] * P
             lg[g] = l_pool.tile([P, GROUP * P, PACK], BF16, align_bytes=64, name="lg")
-            if g % 3 == 1:
-                nc.gpsimd.tensor_scalar(
-                    out=lg[g][:, :toks, :], in0=lt[g][:, :, :toks].rearrange("p t c -> p c t"),
-                    scalar1=1.0, scalar2=0.0, op0=ALU.mult, op1=ALU.add,
-                )
-                return
             nc.scalar.copy(
                 out=lg[g][:, :toks, :].rearrange("p (c i) t -> p c t i", i=4),
                 in_=lt[g][:, :, :toks].rearrange("p t (c i) -> p c t i", i=4),

@@ -26,12 +26,17 @@ FLOPS = 2 * TOKENS * D * (D + D3)
 X_LAG = 0
 XQ_LAG = 1
 Y_LAG = 2
-WQ_LAG = 3
 SQ_LAG = 3
 Z_LAG = 4
 L_LAG = 5
 OUT_LAG = 6
 STORE_LAG = 7
+
+WQ_PERIOD = 3
+SPREAD_PERIOD = 4
+WQ_AFTER = 3
+ROWS_AFTER = 1
+FINE_GROUPS = 2
 
 
 def transpose_rows(nc, banks, copy_out, stage, ident, row_tiles):
@@ -80,27 +85,25 @@ def tile_hlgan_pb_t_kernel(tc, attn_l, wo_l, bo_l, g1, be1, wqkv_g, bqkv_g, out)
                 out=wo_sb[:, 2 * u : 2 * u + 2, :],
                 in_=wo_l[256 * u : 256 * (u + 1), :].rearrange("(q e) k -> q e k", e=2),
             )
-        gb_rows = const.tile([P, 2 * P], BF16)
-        nc.vector.memset(gb_rows[:], 0.0)
-        nc.sync.dma_start(out=gb_rows[0:2, :], in_=g1.rearrange("(u w) -> u w", u=2))
-        nc.sync.dma_start(out=gb_rows[2:4, :], in_=be1.rearrange("(u w) -> u w", u=2))
-        bo_bf = const.tile([P, D], BF16)
-        bq_bf = const.tile([P, D3], BF16)
+        rows = const.tile([P, D + D3 + 2 * P], BF16)
+        nc.vector.memset(rows[:], 0.0)
         wqkv_sb = const.tile([P, D3 // P, D], BF16)
         x_sb = []
         for g in range(n_groups):
             x_g = const.tile([P, sizes[g], D], BF16, name="x_%d" % g)
             nc.sync.dma_start(out=x_g[:], in_=x_dram[:, g * GROUP : g * GROUP + sizes[g], :])
             x_sb.append(x_g)
-            if g == 0:
-                nc.sync.dma_start(out=bo_bf[:], in_=bo_l.partition_broadcast(P))
-            if g == 3:
+            if g == ROWS_AFTER:
+                nc.sync.dma_start(out=rows[0:1, :D], in_=bo_l.rearrange("(o d) -> o d", o=1))
+                nc.sync.dma_start(out=rows[0:1, D : D + D3], in_=bqkv_g.rearrange("(o d) -> o d", o=1))
+                nc.sync.dma_start(out=rows[0:2, D + D3 :], in_=g1.rearrange("(u w) -> u w", u=2))
+                nc.sync.dma_start(out=rows[2:4, D + D3 :], in_=be1.rearrange("(u w) -> u w", u=2))
+            if g == WQ_AFTER:
                 for c in range(3):
                     nc.sync.dma_start(
                         out=wqkv_sb[:, 4 * c : 4 * c + 4, :],
                         in_=wqkv_g[c * BANK : (c + 1) * BANK, :].rearrange("(r q) k -> q r k", q=P),
                     )
-                nc.sync.dma_start(out=bq_bf[:], in_=bqkv_g.partition_broadcast(P))
 
         eps = const.tile([P, 1], F32)
         nc.vector.memset(eps[:], EPS)
@@ -108,6 +111,8 @@ def tile_hlgan_pb_t_kernel(tc, attn_l, wo_l, bo_l, g1, be1, wqkv_g, bqkv_g, out)
         nc.scalar.activation(out=warm[:], in_=eps[:], func=ACT.Abs_reciprocal_sqrt)
         ident = const.tile([P, P], F32)
         make_identity(nc, ident[:])
+        ones = const.tile([P, P], BF16)
+        nc.gpsimd.memset(ones[:], 1.0)
 
         wo_q = const.tile([P, D], U32, align_bytes=64)
         wo_s = const.tile([P, D], U8, align_bytes=64)
@@ -116,26 +121,46 @@ def tile_hlgan_pb_t_kernel(tc, attn_l, wo_l, bo_l, g1, be1, wqkv_g, bqkv_g, out)
             nc, psum_v, nc.vector.tensor_copy, stage, ident, [wo_words[:, r, :] for r in range(4)]
         )
         nc.vector.quantize_mx(out=wo_q[:].bitcast(FP8X4), scales=wo_s[:], in_=wo_grouped[:])
+
         wq_q = const.tile([P, D3], U32, align_bytes=64)
         wq_s = const.tile([P, D3], U8, align_bytes=64)
         wq_words = wqkv_sb[:].bitcast(F32)
-
         bo_bc = const.tile([P, D], F32)
-        nc.vector.tensor_copy(
-            out=bo_bc[:].rearrange("p (u e q) -> p u e q", u=2, e=2),
-            in_=bo_bf[:].rearrange("p (u q e) -> p u e q", u=2, e=2),
-        )
         bq_bc = const.tile([P, D3], F32)
-        nc.gpsimd.tensor_copy(out=bq_bc[:], in_=bq_bf[:])
-
-        gb_bank = psum_v.tile([P, P], F32, tag="bank")
-        nc.tensor.transpose(out=gb_bank[:], in_=gb_rows[:].bitcast(F32), identity=ident[:])
         gain_shift = const.tile([P, 2 * PACK], F32)
-        nc.vector.tensor_copy(out=gain_shift[:], in_=gb_bank[:, 0:4].bitcast(BF16))
 
         x_grouped, xq, xs, yb, ysum, ssq, rstd, nbias, zt, lt, lg, lq, ls, o_sb = (
             {}, {}, {}, {}, {}, {}, {}, {}, {}, {}, {}, {}, {}, {},
         )
+
+        def pack_wqkv(c):
+            cols = slice(c * BANK, (c + 1) * BANK)
+            wq_grouped = transpose_rows(
+                nc, psum_v, nc.vector.tensor_copy, stage, ident, [wq_words[:, 4 * c + r, :] for r in range(4)]
+            )
+            nc.vector.quantize_mx(out=wq_q[:, cols].bitcast(FP8X4), scales=wq_s[:, cols], in_=wq_grouped[:])
+
+        def spread(cols):
+            bank = psum_s.tile([P, BANK], F32, tag="bank")
+            nc.tensor.matmul(out=bank[:], lhsT=ones[:], rhs=rows[:, cols], start=True, stop=True)
+            return bank
+
+        def spread_bo():
+            bank = spread(slice(0, D))
+            nc.scalar.copy(
+                out=bo_bc[:].rearrange("p (u e q) -> p u e q", u=2, e=2),
+                in_=bank[:].rearrange("p (u q e) -> p u e q", u=2, e=2),
+            )
+
+        def spread_bq():
+            for c in range(3):
+                bank = spread(slice(D + c * BANK, D + (c + 1) * BANK))
+                nc.scalar.copy(out=bq_bc[:, c * BANK : (c + 1) * BANK], in_=bank[:])
+
+        def spread_gain_shift():
+            bank = psum_s.tile([P, P], F32, tag="bank")
+            nc.tensor.transpose(out=bank[:], in_=rows[:, D + D3 :].bitcast(F32), identity=ident[:])
+            nc.scalar.copy(out=gain_shift[:], in_=bank[:, 0:4].bitcast(BF16))
 
         def transpose_x(g):
             x_words = x_sb[g][:].bitcast(F32)
@@ -179,7 +204,7 @@ def tile_hlgan_pb_t_kernel(tc, attn_l, wo_l, bo_l, g1, be1, wqkv_g, bqkv_g, out)
                     op0=ALU.mult, op1=ALU.add, accum_out=ysum[g][:, q : q + 1],
                 )
 
-        def row_stds(g):
+        def sum_squares(g):
             ssq[g] = stat.tile([P, GROUP], F32, name="ssq")
             for q in range(sizes[g]):
                 sq = scratch.tile([P, D], BF16, name="sq")
@@ -240,6 +265,9 @@ def tile_hlgan_pb_t_kernel(tc, attn_l, wo_l, bo_l, g1, be1, wqkv_g, bqkv_g, out)
                 in_=lt[g][:, :, :toks].rearrange("p t (c i) -> p c t i", i=4),
             )
 
+        def store(g, q, cols):
+            nc.sync.dma_start(out=out_dram[:, g * GROUP + q, cols], in_=o_sb[g][:, q, cols])
+
         def second_product(g, q, c, banks):
             tok = slice(q * P, (q + 1) * P)
             cols = slice(c * BANK, (c + 1) * BANK)
@@ -259,7 +287,7 @@ def tile_hlgan_pb_t_kernel(tc, attn_l, wo_l, bo_l, g1, be1, wqkv_g, bqkv_g, out)
             cols = slice(c * BANK, (c + 1) * BANK)
             acc = second_product(g, q, c, psum_v)
             nc.vector.tensor_tensor(out=o_sb[g][:, q, cols], in0=acc[:], in1=bq_bc[:, cols], op=ALU.add)
-            if g >= n_groups - 2:
+            if g >= n_groups - FINE_GROUPS:
                 store(g, q, cols)
 
         def out_by_scalar(g, q, c):
@@ -267,30 +295,18 @@ def tile_hlgan_pb_t_kernel(tc, attn_l, wo_l, bo_l, g1, be1, wqkv_g, bqkv_g, out)
             acc = second_product(g, q, c, psum_s)
             nc.scalar.copy(out=o_sb[g][:, q, cols], in_=acc[:])
 
-        def store(g, q, cols):
-            nc.sync.dma_start(out=out_dram[:, g * GROUP + q, cols], in_=o_sb[g][:, q, cols])
-
         def finish_first_tile(g):
             cols = slice(2 * BANK, 3 * BANK)
             nc.gpsimd.tensor_tensor(
                 out=o_sb[g][:, 0, cols], in0=o_sb[g][:, 0, cols], in1=bq_bc[:, cols], op=ALU.add
             )
-            store(g, 0, cols if g >= n_groups - 2 else slice(0, D3))
-
-        def pack_wqkv(c):
-            cols = slice(c * BANK, (c + 1) * BANK)
-            wq_grouped = transpose_rows(
-                nc, psum_v, nc.vector.tensor_copy, stage, ident, [wq_words[:, 4 * c + r, :] for r in range(4)]
-            )
-            nc.vector.quantize_mx(out=wq_q[:, cols].bitcast(FP8X4), scales=wq_s[:, cols], in_=wq_grouped[:])
+            store(g, 0, cols if g >= n_groups - FINE_GROUPS else slice(0, D3))
 
         for period in range(n_groups + STORE_LAG):
 
             def due(lag):
                 return [period - lag] if 0 <= period - lag < n_groups else []
 
-            for g in due(X_LAG):
-                transpose_x(g)
             for g in due(XQ_LAG):
                 quantize_x(g)
             for g in due(Z_LAG):
@@ -298,34 +314,43 @@ def tile_hlgan_pb_t_kernel(tc, attn_l, wo_l, bo_l, g1, be1, wqkv_g, bqkv_g, out)
             for g in due(OUT_LAG):
                 quantize_local(g)
             for g in due(STORE_LAG):
-                if sizes[g] == 2:
+                if sizes[g] == GROUP:
                     out_by_vector(g, 1, 1)
                     out_by_vector(g, 1, 2)
-                    if g < n_groups - 2:
+                    if g < n_groups - FINE_GROUPS:
                         store(g, 1, slice(0, D3))
             for g in due(Z_LAG):
                 normalise(g)
-            for g in due(Y_LAG):
-                first_product(g)
-            if WQ_LAG <= period < WQ_LAG + 3:
-                pack_wqkv(period - WQ_LAG)
+            for g in due(STORE_LAG):
+                if sizes[g] == GROUP:
+                    finish_first_tile(g)
             for g in due(L_LAG):
                 gain_and_shift(g)
             for g in due(SQ_LAG):
-                row_stds(g)
-            for g in due(STORE_LAG):
-                finish_first_tile(g)
+                sum_squares(g)
+            for g in due(X_LAG):
+                transpose_x(g)
+            if period == 0:
+                spread_bo()
+            for g in due(SQ_LAG):
+                reciprocal_stds(g)
+            for g in due(Y_LAG):
+                first_product(g)
+            if WQ_PERIOD <= period < WQ_PERIOD + 3:
+                pack_wqkv(period - WQ_PERIOD)
+            for g in due(L_LAG):
+                regroup(g)
+            if period == SPREAD_PERIOD:
+                spread_gain_shift()
+                spread_bq()
             for g in due(OUT_LAG):
                 o_sb[g] = o_pool.tile([P, GROUP, D3], F32, name="o_sb")
                 out_by_vector(g, 0, 0)
                 out_by_vector(g, 0, 1)
-                if sizes[g] == 2:
+                if sizes[g] == GROUP:
                     out_by_vector(g, 1, 0)
-            for g in due(L_LAG):
-                regroup(g)
-            for g in due(SQ_LAG):
-                reciprocal_stds(g)
-            for g in due(OUT_LAG):
-                out_by_scalar(g, 0, 2)
+                    out_by_scalar(g, 0, 2)
+                else:
+                    out_by_vector(g, 0, 2)
             for g in due(Z_LAG):
                 transpose_z(g)

from contextlib import ExitStack

import concourse.mybir as mybir
from concourse.masks import make_identity

F32 = mybir.dt.float32
BF16 = mybir.dt.bfloat16
U32 = mybir.dt.uint32
U8 = mybir.dt.uint8
FP8X4 = mybir.dt.float8_e4m3fn_x4
ALU = mybir.AluOpType
ACT = mybir.ActivationFunctionType

P = 128
PACK = 4
D = 512
D3 = 1536
BANK = 512
TOKENS = 128 * 37
TILES = TOKENS // P
GROUP = 2
EPS = 1e-5

FLOPS = 2 * TOKENS * D * (D + D3)

X_LAG = 0
XQ_LAG = 1
Y_LAG = 2
SQ_LAG = 3
Z_LAG = 4
L_LAG = 5
OUT_LAG = 6
STORE_LAG = 7

WQ_PERIOD = 3
SPREAD_PERIOD = 4
WQ_AFTER = 3
ROWS_AFTER = 1
FINE_GROUPS = 2


def transpose_rows(nc, banks, copy_out, stage, ident, row_tiles):
    n = len(row_tiles)
    grouped = stage.tile([P, n * P * PACK], BF16, align_bytes=64, tag="grouped")
    words = grouped[:].bitcast(F32).rearrange("p (r u) -> p r u", u=2)
    for first in range(0, n, 2):
        pair = row_tiles[first : first + 2]
        m = len(pair)
        bank = banks.tile([P, 2, 2, P], F32, tag="bank")
        for r in range(m):
            for u in range(2):
                nc.tensor.transpose(
                    out=bank[:, r, u, :], in_=pair[r][:, u * P : (u + 1) * P], identity=ident[:]
                )
        copy_out(
            out=words[:, first * P : (first + m) * P, :].rearrange("p (r c) u -> p r c u", r=m),
            in_=bank[:, :m, :, :].rearrange("p r u c -> p r c u"),
        )
    return grouped


def tile_hlgan_pb_t_kernel(tc, attn_l, wo_l, bo_l, g1, be1, wqkv_g, bqkv_g, out):
    nc = tc.nc
    x_dram = attn_l.flatten_outer_dims().rearrange("(p j) d -> p j d", j=TILES)
    out_dram = out.flatten_outer_dims().rearrange("(p j) f -> p j f", j=TILES)
    sizes = [min(GROUP, TILES - j0) for j0 in range(0, TILES, GROUP)]
    n_groups = len(sizes)

    with ExitStack() as ctx:
        const = ctx.enter_context(tc.tile_pool(name="const", bufs=1))
        stage = ctx.enter_context(tc.tile_pool(name="stage", bufs=4))
        q_pool = ctx.enter_context(tc.tile_pool(name="q", bufs=4))
        y_pool = ctx.enter_context(tc.tile_pool(name="y", bufs=6))
        stat = ctx.enter_context(tc.tile_pool(name="stat", bufs=6))
        scratch = ctx.enter_context(tc.tile_pool(name="scratch", bufs=4))
        l_pool = ctx.enter_context(tc.tile_pool(name="l", bufs=3))
        o_pool = ctx.enter_context(tc.tile_pool(name="o", bufs=4))
        psum_v = ctx.enter_context(tc.psum_pool(name="psum_v", bufs=4))
        psum_s = ctx.enter_context(tc.psum_pool(name="psum_s", bufs=4))
        ctx.enter_context(tc.manual_schedule())

        wo_sb = const.tile([P, 4, D], BF16)
        for u in range(2):
            nc.sync.dma_start(
                out=wo_sb[:, 2 * u : 2 * u + 2, :],
                in_=wo_l[256 * u : 256 * (u + 1), :].rearrange("(q e) k -> q e k", e=2),
            )
        rows = const.tile([P, D + D3 + 2 * P], BF16)
        nc.vector.memset(rows[:], 0.0)
        wqkv_sb = const.tile([P, D3 // P, D], BF16)
        x_sb = []
        for g in range(n_groups):
            x_g = const.tile([P, sizes[g], D], BF16, name="x_%d" % g)
            nc.sync.dma_start(out=x_g[:], in_=x_dram[:, g * GROUP : g * GROUP + sizes[g], :])
            x_sb.append(x_g)
            if g == ROWS_AFTER:
                nc.sync.dma_start(out=rows[0:1, :D], in_=bo_l.rearrange("(o d) -> o d", o=1))
                nc.sync.dma_start(out=rows[0:1, D : D + D3], in_=bqkv_g.rearrange("(o d) -> o d", o=1))
                nc.sync.dma_start(out=rows[0:2, D + D3 :], in_=g1.rearrange("(u w) -> u w", u=2))
                nc.sync.dma_start(out=rows[2:4, D + D3 :], in_=be1.rearrange("(u w) -> u w", u=2))
            if g == WQ_AFTER:
                for c in range(3):
                    nc.sync.dma_start(
                        out=wqkv_sb[:, 4 * c : 4 * c + 4, :],
                        in_=wqkv_g[c * BANK : (c + 1) * BANK, :].rearrange("(r q) k -> q r k", q=P),
                    )

        eps = const.tile([P, 1], F32)
        nc.vector.memset(eps[:], EPS)
        warm = const.tile([P, 1], F32)
        nc.scalar.activation(out=warm[:], in_=eps[:], func=ACT.Abs_reciprocal_sqrt)
        ident = const.tile([P, P], F32)
        make_identity(nc, ident[:])
        ones = const.tile([P, P], BF16)
        nc.gpsimd.memset(ones[:], 1.0)

        wo_q = const.tile([P, D], U32, align_bytes=64)
        wo_s = const.tile([P, D], U8, align_bytes=64)
        wo_words = wo_sb[:].bitcast(F32)
        wo_grouped = transpose_rows(
            nc, psum_v, nc.vector.tensor_copy, stage, ident, [wo_words[:, r, :] for r in range(4)]
        )
        nc.vector.quantize_mx(out=wo_q[:].bitcast(FP8X4), scales=wo_s[:], in_=wo_grouped[:])

        wq_q = const.tile([P, D3], U32, align_bytes=64)
        wq_s = const.tile([P, D3], U8, align_bytes=64)
        wq_words = wqkv_sb[:].bitcast(F32)
        bo_bc = const.tile([P, D], F32)
        bq_bc = const.tile([P, D3], F32)
        gain_shift = const.tile([P, 2 * PACK], F32)

        x_grouped, xq, xs, yb, ysum, ssq, rstd, nbias, zt, lt, lg, lq, ls, o_sb = (
            {}, {}, {}, {}, {}, {}, {}, {}, {}, {}, {}, {}, {}, {},
        )

        def pack_wqkv(c):
            cols = slice(c * BANK, (c + 1) * BANK)
            wq_grouped = transpose_rows(
                nc, psum_v, nc.vector.tensor_copy, stage, ident, [wq_words[:, 4 * c + r, :] for r in range(4)]
            )
            nc.vector.quantize_mx(out=wq_q[:, cols].bitcast(FP8X4), scales=wq_s[:, cols], in_=wq_grouped[:])

        def spread(cols):
            bank = psum_s.tile([P, BANK], F32, tag="bank")
            nc.tensor.matmul(out=bank[:], lhsT=ones[:], rhs=rows[:, cols], start=True, stop=True)
            return bank

        def spread_bo():
            bank = spread(slice(0, D))
            nc.scalar.copy(
                out=bo_bc[:].rearrange("p (u e q) -> p u e q", u=2, e=2),
                in_=bank[:].rearrange("p (u q e) -> p u e q", u=2, e=2),
            )

        def spread_bq():
            for c in range(3):
                bank = spread(slice(D + c * BANK, D + (c + 1) * BANK))
                nc.scalar.copy(out=bq_bc[:, c * BANK : (c + 1) * BANK], in_=bank[:])

        def spread_gain_shift():
            bank = psum_s.tile([P, P], F32, tag="bank")
            nc.tensor.transpose(out=bank[:], in_=rows[:, D + D3 :].bitcast(F32), identity=ident[:])
            nc.scalar.copy(out=gain_shift[:], in_=bank[:, 0:4].bitcast(BF16))

        def transpose_x(g):
            x_words = x_sb[g][:].bitcast(F32)
            x_grouped[g] = transpose_rows(
                nc, psum_s, nc.scalar.copy, stage, ident, [x_words[:, i, :] for i in range(sizes[g])]
            )

        def quantize_x(g):
            toks = sizes[g] * P
            xq[g] = q_pool.tile([P, GROUP * P], U32, align_bytes=64, name="xq")
            xs[g] = q_pool.tile([P, GROUP * P], U8, align_bytes=64, name="xs")
            nc.vector.quantize_mx(
                out=xq[g][:, :toks].bitcast(FP8X4), scales=xs[g][:, :toks], in_=x_grouped[g][:]
            )

        def quantize_local(g):
            toks = sizes[g] * P
            lq[g] = q_pool.tile([P, GROUP * P], U32, align_bytes=64, name="lq")
            ls[g] = q_pool.tile([P, GROUP * P], U8, align_bytes=64, name="ls")
            nc.vector.quantize_mx(
                out=lq[g][:, :toks].bitcast(FP8X4), scales=ls[g][:, :toks],
                in_=lg[g][:, :toks, :].rearrange("p c t -> p (c t)"),
            )

        def first_product(g):
            yb[g] = y_pool.tile([P, GROUP, D], F32, name="yb")
            ysum[g] = stat.tile([P, GROUP], F32, name="ysum")
            for q in range(sizes[g]):
                y_ps = psum_v.tile([P, BANK], F32, tag="bank")
                nc.tensor.matmul_mx(
                    out=y_ps[:],
                    lhsT=xq[g][:, q * P : (q + 1) * P].bitcast(FP8X4),
                    lhsT_scale=xs[g][:, q * P : (q + 1) * P],
                    rhs=wo_q[:].bitcast(FP8X4),
                    rhs_scale=wo_s[:],
                    start=True,
                    stop=True,
                )
                nc.vector.scalar_tensor_tensor(
                    out=yb[g][:, q, :], in0=y_ps[:], scalar=1.0, in1=bo_bc[:],
                    op0=ALU.mult, op1=ALU.add, accum_out=ysum[g][:, q : q + 1],
                )

        def sum_squares(g):
            ssq[g] = stat.tile([P, GROUP], F32, name="ssq")
            for q in range(sizes[g]):
                sq = scratch.tile([P, D], BF16, name="sq")
                nc.scalar.activation(
                    out=sq[:], in_=yb[g][:, q, :], func=ACT.Square,
                    bias=ysum[g][:, q : q + 1], scale=-float(D), accum_out=ssq[g][:, q : q + 1],
                )

        def reciprocal_stds(g):
            n = sizes[g]
            rstd[g] = stat.tile([P, GROUP], F32, name="rstd")
            nc.scalar.activation(
                out=rstd[g][:, :n], in_=ssq[g][:, :n], func=ACT.Abs_reciprocal_sqrt, bias=eps[:], scale=1.0 / D**3
            )

        def scaled_means(g):
            n = sizes[g]
            nbias[g] = stat.tile([P, GROUP], F32, name="nbias")
            nc.vector.scalar_tensor_tensor(
                out=nbias[g][:, :n], in0=ysum[g][:, :n], scalar=-1.0 / D, in1=rstd[g][:, :n],
                op0=ALU.mult, op1=ALU.mult,
            )

        def normalise(g):
            for q in range(sizes[g]):
                nc.gpsimd.tensor_scalar(
                    out=yb[g][:, q, :], in0=yb[g][:, q, :],
                    scalar1=rstd[g][:, q : q + 1], scalar2=nbias[g][:, q : q + 1],
                    op0=ALU.mult, op1=ALU.add,
                )

        def transpose_z(g):
            for h in range(2):
                bank = psum_s.tile([P, 2, GROUP * P], F32, tag="bank")
                zt[g, h] = bank
                for k in range(2):
                    t = 2 * h + k
                    for i in range(sizes[g]):
                        nc.tensor.transpose(
                            out=bank[:, k, i * P : (i + 1) * P], in_=yb[g][:, i, t * P : (t + 1) * P],
                            identity=ident[:],
                        )

        def gain_and_shift(g):
            toks = sizes[g] * P
            lt[g] = l_pool.tile([P, PACK, GROUP * P], BF16, name="lt")
            for t in range(PACK):
                nc.scalar.activation(
                    out=lt[g][:, t, :toks], in_=zt[g, t // 2][:, t % 2, :toks], func=ACT.Identity,
                    bias=gain_shift[:, PACK + t : PACK + t + 1], scale=gain_shift[:, t : t + 1],
                )

        def regroup(g):
            toks = sizes[g] * P
            lg[g] = l_pool.tile([P, GROUP * P, PACK], BF16, align_bytes=64, name="lg")
            nc.scalar.copy(
                out=lg[g][:, :toks, :].rearrange("p (c i) t -> p c t i", i=4),
                in_=lt[g][:, :, :toks].rearrange("p t (c i) -> p c t i", i=4),
            )

        def store(g, q, cols):
            nc.sync.dma_start(out=out_dram[:, g * GROUP + q, cols], in_=o_sb[g][:, q, cols])

        def second_product(g, q, c, banks):
            tok = slice(q * P, (q + 1) * P)
            cols = slice(c * BANK, (c + 1) * BANK)
            acc = banks.tile([P, BANK], F32, tag="bank")
            nc.tensor.matmul_mx(
                out=acc[:],
                lhsT=lq[g][:, tok].bitcast(FP8X4),
                lhsT_scale=ls[g][:, tok],
                rhs=wq_q[:, cols].bitcast(FP8X4),
                rhs_scale=wq_s[:, cols],
                start=True,
                stop=True,
            )
            return acc

        def out_by_vector(g, q, c):
            cols = slice(c * BANK, (c + 1) * BANK)
            acc = second_product(g, q, c, psum_v)
            nc.vector.tensor_tensor(out=o_sb[g][:, q, cols], in0=acc[:], in1=bq_bc[:, cols], op=ALU.add)
            if g >= n_groups - FINE_GROUPS:
                store(g, q, cols)

        def out_by_scalar(g, q, c):
            cols = slice(c * BANK, (c + 1) * BANK)
            acc = second_product(g, q, c, psum_s)
            nc.scalar.copy(out=o_sb[g][:, q, cols], in_=acc[:])

        def finish_first_tile(g):
            cols = slice(2 * BANK, 3 * BANK)
            nc.gpsimd.tensor_tensor(
                out=o_sb[g][:, 0, cols], in0=o_sb[g][:, 0, cols], in1=bq_bc[:, cols], op=ALU.add
            )
            store(g, 0, cols if g >= n_groups - FINE_GROUPS else slice(0, D3))

        for period in range(n_groups + STORE_LAG):

            def due(lag):
                return [period - lag] if 0 <= period - lag < n_groups else []

            for g in due(XQ_LAG):
                quantize_x(g)
            for g in due(Z_LAG):
                scaled_means(g)
            for g in due(OUT_LAG):
                quantize_local(g)
            for g in due(STORE_LAG):
                if sizes[g] == GROUP:
                    out_by_vector(g, 1, 1)
                    out_by_vector(g, 1, 2)
                    if g < n_groups - FINE_GROUPS:
                        store(g, 1, slice(0, D3))
            for g in due(Z_LAG):
                normalise(g)
            for g in due(STORE_LAG):
                if sizes[g] == GROUP:
                    finish_first_tile(g)
            for g in due(L_LAG):
                gain_and_shift(g)
            for g in due(SQ_LAG):
                sum_squares(g)
            for g in due(X_LAG):
                transpose_x(g)
            if period == 0:
                spread_bo()
            for g in due(SQ_LAG):
                reciprocal_stds(g)
            for g in due(Y_LAG):
                first_product(g)
            if WQ_PERIOD <= period < WQ_PERIOD + 3:
                pack_wqkv(period - WQ_PERIOD)
            for g in due(L_LAG):
                regroup(g)
            if period == SPREAD_PERIOD:
                spread_gain_shift()
                spread_bq()
            for g in due(OUT_LAG):
                o_sb[g] = o_pool.tile([P, GROUP, D3], F32, name="o_sb")
                out_by_vector(g, 0, 0)
                out_by_vector(g, 0, 1)
                if sizes[g] == GROUP:
                    out_by_vector(g, 1, 0)
                    out_by_scalar(g, 0, 2)
                else:
                    out_by_vector(g, 0, 2)
            for g in due(Z_LAG):
                transpose_z(g)
